import numpy as np
import ml_dtypes


def mxq(x, axis, fmt="e4m3"):
    dtype, down = {"e4m3": (ml_dtypes.float8_e4m3fn, 7), "e5m2": (ml_dtypes.float8_e5m2, 14)}[fmt]
    v = np.moveaxis(np.asarray(x, np.float32).astype(ml_dtypes.bfloat16).astype(np.float64), axis, -1)
    blocks = v.reshape(v.shape[:-1] + (-1, 32))
    amax = np.abs(blocks).max(-1, keepdims=True)
    byte = np.maximum(np.where(amax > 0, np.frexp(amax)[1] - 1 + 127, 0) - down, 1)
    scale = np.exp2(byte - 127.0)
    codes = (blocks / scale).astype(np.float32).astype(dtype).astype(np.float64)
    return np.moveaxis((codes * scale).reshape(v.shape), -1, axis)


WIDE = False


def mx_kscale(k):
    if not WIDE:
        return np.ones(k)
    levels = np.array([10, -10, 5, -5, 0])
    if k % 512:
        return np.exp2(np.random.permutation(np.resize(levels, k // 32))).repeat(32)
    a = np.empty((k // 512, 16))
    for p in range(k // 512):
        a[p, :8] = np.random.permutation(np.resize(levels, 8))
        for g in range(8):
            far = levels[np.abs(levels - a[p, g]) >= 10]
            a[p, g + 8] = far[np.random.randint(len(far))]
    return np.exp2(a.ravel()).repeat(32)


BF16 = ml_dtypes.bfloat16


def bf(x):
    return np.asarray(x, np.float32).astype(BF16)


def f64(x):
    return np.asarray(x).astype(np.float64)


B, S, C, H, D = 2, 256, 256, 8, 128
E = H * D
EPS = 1e-15


def setup_inputs():
    t = mx_kscale(E)
    return {"q_feat": bf(np.maximum(np.random.standard_normal((B, H, S, D)), 0.0)),
            "vk": bf(np.random.standard_normal((B, H, D, D)) * np.sqrt(S) * t.reshape(H, D)[None, :, :, None]),
            "k_sum": bf(S * (0.11 + 0.02 * np.random.standard_normal((B, H, D)))),
            "Wo": bf(np.random.standard_normal((C, E)) * 6.0 / np.sqrt(E) / t[None, :]),
            "bo": bf(np.random.standard_normal(C) * 0.1)}


def reference(q_feat, vk, k_sum, Wo, bo):
    hs = f64(vk) @ f64(q_feat).transpose(0, 1, 3, 2)
    den = (f64(q_feat) * f64(k_sum)[:, :, None, :]).sum(-1)
    hs = hs / (den[:, :, None, :] + EPS)
    a = hs.transpose(0, 3, 1, 2).reshape(B, S, E)
    return (mxq(a, 2, "e4m3") @ mxq(f64(Wo), 1, "e4m3").T) + f64(bo)

@@ -1,0 +1,172 @@
+import concourse.mybir as mybir
+from concourse.masks import make_identity
+
+F32 = mybir.dt.float32
+BF16 = mybir.dt.bfloat16
+U32 = mybir.dt.uint32
+U8 = mybir.dt.uint8
+FP8X4 = mybir.dt.float8_e4m3fn_x4
+MULT = mybir.AluOpType.mult
+ADD = mybir.AluOpType.add
+
+P = 128
+PACK = 4
+B, H, S, D, C = 2, 8, 256, 128, 256
+EPS = 1e-15
+TOKEN_TILES = S // P
+GROUPS = H // PACK
+UNITS = B * GROUPS
+C_TILES = C // P
+HALVES = 2
+ROWS = D // PACK
+
+FLOPS = 2 * B * H * S * D * D + 2 * B * H * S * D + 2 * B * S * H * D * C
+
+
+def tile_lineartransformerblock_pc_s_kernel(tc, q_feat, vk, k_sum, Wo, bo, out):
+    nc = tc.nc
+    with tc.tile_pool(name="keep", bufs=1) as keep, tc.psum_pool(name="psum", bufs=2) as psum:
+        ks_rows = keep.tile([P, D], BF16)
+        nc.vector.memset(ks_rows[:], 0.0)
+        nc.sync.dma_start(out=ks_rows[0 : B * H, :], in_=k_sum.rearrange("b h d -> (b h) d"))
+
+        vk_sb = [keep.tile([P, PACK, D], BF16, name="vk_sb%d" % u) for u in range(UNITS)]
+        q_sb = [keep.tile([P, PACK, TOKEN_TILES, D], BF16, name="q_sb%d" % u) for u in range(UNITS)]
+        wo_sb = keep.tile([P, C_TILES, H * D], BF16)
+        bias = keep.tile([P, C], BF16)
+
+        def load_unit(u):
+            b, g = divmod(u, GROUPS)
+            heads = slice(PACK * g, PACK * (g + 1))
+            nc.sync.dma_start(out=vk_sb[u][:], in_=vk[b, heads].rearrange("h n d -> n h d"))
+            nc.sync.dma_start(out=q_sb[u][:], in_=q_feat[b, heads].rearrange("h (p j) d -> p h j d", j=TOKEN_TILES))
+
+        load_unit(0)
+        load_unit(1)
+        nc.sync.dma_start(out=wo_sb[:], in_=Wo.rearrange("(ct p) k -> p ct k", p=P))
+        for u in range(2, UNITS):
+            load_unit(u)
+        nc.sync.dma_start(out=bias[:], in_=bo.partition_broadcast(P))
+
+        ident = keep.tile([P, P], BF16)
+        make_identity(nc, ident[:])
+        ident_f32 = keep.tile([P, P], F32)
+        make_identity(nc, ident_f32[:])
+
+        ksT_ps = psum.tile([P, PACK, P], BF16, tag="tin", bufs=3)
+        nc.tensor.transpose(ksT_ps[:, 0, :], ks_rows[:], ident[:])
+        ksT = keep.tile([P, B * H], BF16)
+        nc.scalar.copy(out=ksT[:], in_=ksT_ps[:, 0, 0 : B * H])
+
+        vkT = [keep.tile([P, PACK, D], BF16, name="vkT%d" % u) for u in range(UNITS)]
+        qT = [keep.tile([P, TOKEN_TILES, PACK, P], BF16, name="qT%d" % u) for u in range(UNITS)]
+        a_sb = [keep.tile([P, TOKEN_TILES, PACK, PACK, ROWS], BF16, name="a_sb%d" % u) for u in range(UNITS)]
+        a_grouped = [keep.tile([P, TOKEN_TILES, P, PACK], BF16, name="a_grouped%d" % u, align_bytes=64) for u in range(UNITS)]
+        a_codes = [keep.tile([P, TOKEN_TILES, P], U32, name="a_codes%d" % u, align_bytes=64) for u in range(UNITS)]
+        a_scales = [keep.tile([P, TOKEN_TILES, P], U8, name="a_scales%d" % u, align_bytes=64) for u in range(UNITS)]
+        w_grouped = keep.tile([P, GROUPS, C, PACK], BF16, align_bytes=64)
+        w_codes = keep.tile([P, GROUPS, C], U32, align_bytes=64)
+        w_scales = keep.tile([P, GROUPS, C], U8, align_bytes=64)
+
+        def transpose_inputs(u):
+            vkT_ps = psum.tile([P, PACK, P], BF16, tag="tin", bufs=3)
+            for t in range(PACK):
+                nc.tensor.transpose(vkT_ps[:, t, :], vk_sb[u][:, t, :], ident[:])
+            nc.scalar.copy(out=vkT[u][:], in_=vkT_ps[:])
+            for j in range(TOKEN_TILES):
+                qT_ps = psum.tile([P, PACK, P], BF16, tag="tin", bufs=3)
+                for t in range(PACK):
+                    nc.tensor.transpose(qT_ps[:, t, :], q_sb[u][:, t, j, :], ident[:])
+                nc.scalar.copy(out=qT[u][:, j, :, :], in_=qT_ps[:])
+
+        def quantise_wo():
+            wo_words = wo_sb[:].bitcast(F32)
+            for g in range(GROUPS):
+                woT_ps = psum.tile([P, HALVES, C], F32, tag="tin", bufs=3)
+                for w in range(HALVES):
+                    first = HALVES * g * P + w
+                    for ct in range(C_TILES):
+                        nc.tensor.transpose(
+                            woT_ps[:, w, P * ct : P * (ct + 1)], wo_words[:, ct, first : HALVES * (g + 1) * P : HALVES], ident_f32[:]
+                        )
+                nc.vector.tensor_copy(out=w_grouped[:, g, :, :].bitcast(F32), in_=woT_ps[:].rearrange("p w c -> p c w"))
+            nc.vector.quantize_mx(
+                out=w_codes[:].rearrange("n g c -> n (g c)").bitcast(FP8X4),
+                scales=w_scales[:].rearrange("n g c -> n (g c)"),
+                in_=w_grouped[:].rearrange("n g c t -> n (g c t)"),
+            )
+
+        recip = [keep.tile([P, TOKEN_TILES, PACK], F32, name="recip%d" % u) for u in range(UNITS)]
+
+        def denominators(u):
+            den_ps = psum.tile([P, TOKEN_TILES, PACK], F32, tag="den", bufs=1)
+            for j in range(TOKEN_TILES):
+                for t in range(PACK):
+                    bh = PACK * u + t
+                    nc.tensor.matmul(
+                        out=den_ps[:, j, t : t + 1], lhsT=qT[u][:, j, t, :], rhs=ksT[:, bh : bh + 1], start=True, stop=True
+                    )
+            den = keep.tile([P, TOKEN_TILES, PACK], F32, name="den%d" % u)
+            nc.vector.tensor_scalar_add(out=den[:], in0=den_ps[:], scalar1=EPS)
+            nc.vector.reciprocal(out=recip[u][:], in_=den[:])
+
+        def read_out(u):
+            for j in range(TOKEN_TILES):
+                hs_ps = psum.tile([P, PACK, PACK, ROWS], F32, tag="hs")
+                for t in range(PACK):
+                    nc.tensor.matmul(
+                        out=hs_ps[:, :, t, :],
+                        lhsT=qT[u][:, j, t, :],
+                        rhs=vkT[u][:, t, :].rearrange("d (m i) -> d i m", i=PACK),
+                        start=True,
+                        stop=True,
+                    )
+                nc.vector.tensor_tensor(
+                    out=a_sb[u][:, j, :, :, :],
+                    in0=hs_ps[:],
+                    in1=recip[u][:, j, :].unsqueeze(1).unsqueeze(3).to_broadcast([P, PACK, PACK, ROWS]),
+                    op=MULT,
+                )
+
+        def quantise_a(u):
+            for j in range(TOKEN_TILES):
+                aT_ps = psum.tile([P, PACK, P], BF16, tag="aT")
+                for t in range(PACK):
+                    nc.tensor.transpose(aT_ps[:, t, :], a_sb[u][:, j, t, :, :].rearrange("p h m -> p (h m)"), ident[:])
+                nc.scalar.copy(out=a_grouped[u][:, j, :, :], in_=aT_ps[:].rearrange("n t p -> n p t"))
+                nc.vector.quantize_mx(
+                    out=a_codes[u][:, j, :].bitcast(FP8X4),
+                    scales=a_scales[u][:, j, :],
+                    in_=a_grouped[u][:, j, :, :].rearrange("n p t -> n (p t)"),
+                )
+
+        def project(b, j):
+            out_ps = psum.tile([P, C], F32, tag="hs")
+            for g in range(GROUPS):
+                u = GROUPS * b + g
+                nc.tensor.matmul_mx(
+                    out=out_ps[:],
+                    lhsT=a_codes[u][:, j, :].bitcast(FP8X4),
+                    lhsT_scale=a_scales[u][:, j, :],
+                    rhs=w_codes[:, g, :].bitcast(FP8X4),
+                    rhs_scale=w_scales[:, g, :],
+                    start=(g == 0),
+                    stop=(g == GROUPS - 1),
+                )
+            out_sb = keep.tile([P, C], F32, name="out_sb%d%d" % (b, j))
+            nc.vector.tensor_tensor(out=out_sb[:], in0=out_ps[:], in1=bias[:], op=ADD)
+            nc.sync.dma_start(out=out[b].rearrange("(p j) c -> p j c", j=TOKEN_TILES)[:, j, :], in_=out_sb[:])
+
+        for step in range(UNITS + 2):
+            if step < UNITS:
+                transpose_inputs(step)
+                denominators(step)
+            if 1 <= step <= UNITS:
+                read_out(step - 1)
+            if step == 1:
+                quantise_wo()
+            if step >= 2:
+                quantise_a(step - 2)
+        for b in range(B):
+            for j in range(TOKEN_TILES):
+                project(b, j)

@@ -13,12 +13,14 @@ P = 128
 PACK = 4
 B, H, S, D, C = 2, 8, 256, 128, 256
 EPS = 1e-15
-TOKEN_TILES = S // P
 GROUPS = H // PACK
 UNITS = B * GROUPS
+PH = P // PACK
+RUN = S // PH
+TOKEN_TILES = S // P
+PER = RUN // TOKEN_TILES
 C_TILES = C // P
 HALVES = 2
-ROWS = D // PACK
 
 FLOPS = 2 * B * H * S * D * D + 2 * B * H * S * D + 2 * B * S * H * D * C
 
@@ -31,19 +33,21 @@ def tile_lineartransformerblock_pc_s_kernel(tc, q_feat, vk, k_sum, Wo, bo, out):
         nc.sync.dma_start(out=ks_rows[0 : B * H, :], in_=k_sum.rearrange("b h d -> (b h) d"))
 
         vk_sb = [keep.tile([P, PACK, D], BF16, name="vk_sb%d" % u) for u in range(UNITS)]
-        q_sb = [keep.tile([P, PACK, TOKEN_TILES, D], BF16, name="q_sb%d" % u) for u in range(UNITS)]
+        q_sb = [keep.tile([P, RUN, D], BF16, name="q_sb%d" % u) for u in range(UNITS)]
         wo_sb = keep.tile([P, C_TILES, H * D], BF16)
         bias = keep.tile([P, C], BF16)
+        vk_rows = vk.rearrange("b h n d -> (b h n) d")
+        q_rows = q_feat.rearrange("b h s d -> (b h s) d")
 
         def load_unit(u):
-            b, g = divmod(u, GROUPS)
-            heads = slice(PACK * g, PACK * (g + 1))
-            nc.sync.dma_start(out=vk_sb[u][:], in_=vk[b, heads].rearrange("h n d -> n h d"))
-            nc.sync.dma_start(out=q_sb[u][:], in_=q_feat[b, heads].rearrange("h (p j) d -> p h j d", j=TOKEN_TILES))
+            vk_unit = vk_rows[PACK * D * u : PACK * D * (u + 1), :]
+            nc.sync.dma_start(out=vk_sb[u][:], in_=vk_unit.rearrange("(p i) d -> p i d", i=PACK))
+            q_unit = q_rows[PACK * S * u : PACK * S * (u + 1), :]
+            nc.sync.dma_start(out=q_sb[u][:], in_=q_unit.rearrange("(p r) d -> p r d", r=RUN))
 
         load_unit(0)
         load_unit(1)
-        nc.sync.dma_start(out=wo_sb[:], in_=Wo.rearrange("(ct p) k -> p ct k", p=P))
+        nc.sync.dma_start(out=wo_sb[:], in_=Wo.rearrange("(p ct) k -> p ct k", ct=C_TILES))
         for u in range(2, UNITS):
             load_unit(u)
         nc.sync.dma_start(out=bias[:], in_=bo.partition_broadcast(P))
@@ -52,15 +56,19 @@ def tile_lineartransformerblock_pc_s_kernel(tc, q_feat, vk, k_sum, Wo, bo, out):
         make_identity(nc, ident[:])
         ident_f32 = keep.tile([P, P], F32)
         make_identity(nc, ident_f32[:])
+        sort_f32 = keep.tile([P, P], F32)
+        nc.gpsimd.tensor_copy(
+            out=sort_f32[:].rearrange("k (p jj) -> k p jj", jj=PER), in_=ident_f32[:].rearrange("k (jj p) -> k p jj", jj=PER)
+        )
 
-        ksT_ps = psum.tile([P, PACK, P], BF16, tag="tin", bufs=3)
-        nc.tensor.transpose(ksT_ps[:, 0, :], ks_rows[:], ident[:])
+        ksT_ps = psum.tile([P, PACK * P], BF16, tag="tin", bufs=3)
+        nc.tensor.transpose(ksT_ps[:, 0:P], ks_rows[:], ident[:])
         ksT = keep.tile([P, B * H], BF16)
-        nc.scalar.copy(out=ksT[:], in_=ksT_ps[:, 0, 0 : B * H])
+        nc.scalar.copy(out=ksT[:], in_=ksT_ps[:, 0 : B * H])
 
-        vkT = [keep.tile([P, PACK, D], BF16, name="vkT%d" % u) for u in range(UNITS)]
-        qT = [keep.tile([P, TOKEN_TILES, PACK, P], BF16, name="qT%d" % u) for u in range(UNITS)]
-        a_sb = [keep.tile([P, TOKEN_TILES, PACK, PACK, ROWS], BF16, name="a_sb%d" % u) for u in range(UNITS)]
+        vkT = [keep.tile([P, PACK, PACK, PH], BF16, name="vkT%d" % u) for u in range(UNITS)]
+        qT = [keep.tile([P, TOKEN_TILES, PACK, PER, PH], BF16, name="qT%d" % u) for u in range(UNITS)]
+        a_sb = [keep.tile([P, TOKEN_TILES, HALVES, PACK * D // HALVES], BF16, name="a_sb%d" % u) for u in range(UNITS)]
         a_grouped = [keep.tile([P, TOKEN_TILES, P, PACK], BF16, name="a_grouped%d" % u, align_bytes=64) for u in range(UNITS)]
         a_codes = [keep.tile([P, TOKEN_TILES, P], U32, name="a_codes%d" % u, align_bytes=64) for u in range(UNITS)]
         a_scales = [keep.tile([P, TOKEN_TILES, P], U8, name="a_scales%d" % u, align_bytes=64) for u in range(UNITS)]
@@ -69,75 +77,83 @@ def tile_lineartransformerblock_pc_s_kernel(tc, q_feat, vk, k_sum, Wo, bo, out):
         w_scales = keep.tile([P, GROUPS, C], U8, align_bytes=64)
 
         def transpose_inputs(u):
-            vkT_ps = psum.tile([P, PACK, P], BF16, tag="tin", bufs=3)
-            for t in range(PACK):
-                nc.tensor.transpose(vkT_ps[:, t, :], vk_sb[u][:, t, :], ident[:])
+            vkT_ps = psum.tile([P, PACK, PACK, PH], BF16, tag="tin", bufs=3)
+            for i in range(PACK):
+                nc.tensor.transpose(vkT_ps[:, :, i, :], vk_sb[u][:, i, :], ident[:])
             nc.scalar.copy(out=vkT[u][:], in_=vkT_ps[:])
             for j in range(TOKEN_TILES):
-                qT_ps = psum.tile([P, PACK, P], BF16, tag="tin", bufs=3)
-                for t in range(PACK):
-                    nc.tensor.transpose(qT_ps[:, t, :], q_sb[u][:, t, j, :], ident[:])
-                nc.scalar.copy(out=qT[u][:, j, :, :], in_=qT_ps[:])
+                qT_ps = psum.tile([P, PACK, PER, PH], BF16, tag="tin", bufs=3)
+                for jj in range(PER):
+                    nc.tensor.transpose(qT_ps[:, :, jj, :], q_sb[u][:, TOKEN_TILES * jj + j, :], ident[:])
+                nc.scalar.copy(out=qT[u][:, j], in_=qT_ps[:])
 
         def quantise_wo():
             wo_words = wo_sb[:].bitcast(F32)
             for g in range(GROUPS):
-                woT_ps = psum.tile([P, HALVES, C], F32, tag="tin", bufs=3)
+                woT_ps = psum.tile([P, HALVES, C_TILES, P], F32, tag="tin", bufs=3)
                 for w in range(HALVES):
-                    first = HALVES * g * P + w
                     for ct in range(C_TILES):
-                        nc.tensor.transpose(
-                            woT_ps[:, w, P * ct : P * (ct + 1)], wo_words[:, ct, first : HALVES * (g + 1) * P : HALVES], ident_f32[:]
-                        )
-                nc.vector.tensor_copy(out=w_grouped[:, g, :, :].bitcast(F32), in_=woT_ps[:].rearrange("p w c -> p c w"))
+                        every_second = wo_words[:, ct, HALVES * P * g + w : HALVES * P * (g + 1) : HALVES]
+                        nc.tensor.transpose(woT_ps[:, w, ct, :], every_second, ident_f32[:])
+                nc.vector.tensor_copy(
+                    out=w_grouped[:, g].rearrange("n c t -> n (c t)").bitcast(F32).rearrange("n (p ct w) -> n p ct w", ct=C_TILES, w=HALVES),
+                    in_=woT_ps[:].rearrange("n w ct p -> n p ct w"),
+                )
             nc.vector.quantize_mx(
                 out=w_codes[:].rearrange("n g c -> n (g c)").bitcast(FP8X4),
                 scales=w_scales[:].rearrange("n g c -> n (g c)"),
                 in_=w_grouped[:].rearrange("n g c t -> n (g c t)"),
             )
 
-        recip = [keep.tile([P, TOKEN_TILES, PACK], F32, name="recip%d" % u) for u in range(UNITS)]
+        recip = [keep.tile([P, TOKEN_TILES, HALVES, PACK], F32, name="recip%d" % u) for u in range(UNITS)]
 
         def denominators(u):
             den_ps = psum.tile([P, TOKEN_TILES, PACK], F32, tag="den", bufs=1)
             for j in range(TOKEN_TILES):
-                for t in range(PACK):
-                    bh = PACK * u + t
+                for h in range(PACK):
+                    bh = PACK * u + h
                     nc.tensor.matmul(
-                        out=den_ps[:, j, t : t + 1], lhsT=qT[u][:, j, t, :], rhs=ksT[:, bh : bh + 1], start=True, stop=True
+                        out=den_ps[:, j, h : h + 1],
+                        lhsT=qT[u][:, j, h].rearrange("d jj p -> d (jj p)"),
+                        rhs=ksT[:, bh : bh + 1],
+                        start=True,
+                        stop=True,
                     )
             den = keep.tile([P, TOKEN_TILES, PACK], F32, name="den%d" % u)
             nc.vector.tensor_scalar_add(out=den[:], in0=den_ps[:], scalar1=EPS)
-            nc.vector.reciprocal(out=recip[u][:], in_=den[:])
+            nc.vector.reciprocal(out=recip[u][:], in_=den[:].unsqueeze(2).to_broadcast([P, TOKEN_TILES, HALVES, PACK]))
 
         def read_out(u):
             for j in range(TOKEN_TILES):
-                hs_ps = psum.tile([P, PACK, PACK, ROWS], F32, tag="hs")
-                for t in range(PACK):
+                hs_ps = psum.tile([P, HALVES, PACK, HALVES, PH], F32, tag="hs")
+                for h in range(PACK):
                     nc.tensor.matmul(
-                        out=hs_ps[:, :, t, :],
-                        lhsT=qT[u][:, j, t, :],
-                        rhs=vkT[u][:, t, :].rearrange("d (m i) -> d i m", i=PACK),
+                        out=hs_ps[:, :, h, :, :],
+                        lhsT=qT[u][:, j, h].rearrange("d jj p -> d (jj p)"),
+                        rhs=vkT[u][:, h].rearrange("d (w e) m -> d w e m", w=HALVES),
                         start=True,
                         stop=True,
                     )
                 nc.vector.tensor_tensor(
-                    out=a_sb[u][:, j, :, :, :],
-                    in0=hs_ps[:],
-                    in1=recip[u][:, j, :].unsqueeze(1).unsqueeze(3).to_broadcast([P, PACK, PACK, ROWS]),
+                    out=a_sb[u][:, j].rearrange("p w (h m e) -> p (w h) m e", h=PACK, e=HALVES),
+                    in0=hs_ps[:].rearrange("p w h e m -> p (w h) m e"),
+                    in1=recip[u][:, j].rearrange("p w h -> p (w h)").unsqueeze(2).unsqueeze(3).to_broadcast([P, HALVES * PACK, PH, HALVES]),
                     op=MULT,
                 )
 
         def quantise_a(u):
             for j in range(TOKEN_TILES):
-                aT_ps = psum.tile([P, PACK, P], BF16, tag="aT")
-                for t in range(PACK):
-                    nc.tensor.transpose(aT_ps[:, t, :], a_sb[u][:, j, t, :, :].rearrange("p h m -> p (h m)"), ident[:])
-                nc.scalar.copy(out=a_grouped[u][:, j, :, :], in_=aT_ps[:].rearrange("n t p -> n p t"))
+                aT_ps = psum.tile([P, HALVES, P], F32, tag="aT")
+                for w in range(HALVES):
+                    nc.tensor.transpose(aT_ps[:, w, :], a_sb[u][:, j, w, :].bitcast(F32), sort_f32[:])
+                nc.scalar.copy(
+                    out=a_grouped[u][:, j].rearrange("n q t -> n (q t)").bitcast(F32).rearrange("n (q w) -> n q w", w=HALVES),
+                    in_=aT_ps[:].rearrange("n w q -> n q w"),
+                )
                 nc.vector.quantize_mx(
                     out=a_codes[u][:, j, :].bitcast(FP8X4),
                     scales=a_scales[u][:, j, :],
-                    in_=a_grouped[u][:, j, :, :].rearrange("n p t -> n (p t)"),
+                    in_=a_grouped[u][:, j, :, :].rearrange("n q t -> n (q t)"),
                 )
 
         def project(b, j):
@@ -155,7 +171,7 @@ def tile_lineartransformerblock_pc_s_kernel(tc, q_feat, vk, k_sum, Wo, bo, out):
                 )
             out_sb = keep.tile([P, C], F32, name="out_sb%d%d" % (b, j))
             nc.vector.tensor_tensor(out=out_sb[:], in0=out_ps[:], in1=bias[:], op=ADD)
-            nc.sync.dma_start(out=out[b].rearrange("(p j) c -> p j c", j=TOKEN_TILES)[:, j, :], in_=out_sb[:])
+            nc.sync.dma_start(out=out[b].rearrange("(q j) c -> q j c", j=TOKEN_TILES)[:, j, :], in_=out_sb[:])
 
         for step in range(UNITS + 2):
             if step < UNITS:

@@ -8,6 +8,7 @@ U8 = mybir.dt.uint8
 FP8X4 = mybir.dt.float8_e4m3fn_x4
 MULT = mybir.AluOpType.mult
 ADD = mybir.AluOpType.add
+COPY = mybir.ActivationFunctionType.Copy
 
 P = 128
 PACK = 4
@@ -27,7 +28,7 @@ FLOPS = 2 * B * H * S * D * D + 2 * B * H * S * D + 2 * B * S * H * D * C
 
 def tile_lineartransformerblock_pc_s_kernel(tc, q_feat, vk, k_sum, Wo, bo, out):
     nc = tc.nc
-    with tc.tile_pool(name="keep", bufs=1) as keep, tc.psum_pool(name="psum", bufs=2) as psum:
+    with tc.tile_pool(name="keep", bufs=1) as keep, tc.psum_pool(name="psum", bufs=1) as psum:
         ks_rows = keep.tile([P, D], BF16)
         nc.vector.memset(ks_rows[:], 0.0)
         nc.sync.dma_start(out=ks_rows[0 : B * H, :], in_=k_sum.rearrange("b h d -> (b h) d"))
@@ -76,92 +77,106 @@ def tile_lineartransformerblock_pc_s_kernel(tc, q_feat, vk, k_sum, Wo, bo, out):
         w_codes = keep.tile([P, GROUPS, C], U32, align_bytes=64)
         w_scales = keep.tile([P, GROUPS, C], U8, align_bytes=64)
 
-        def transpose_inputs(u):
-            vkT_ps = psum.tile([P, PACK, PACK, PH], BF16, tag="tin", bufs=3)
+        den = [keep.tile([P, TOKEN_TILES, PACK], F32, name="den%d" % u) for u in range(UNITS)]
+        recip = [keep.tile([P, TOKEN_TILES, HALVES, PACK], F32, name="recip%d" % u) for u in range(UNITS)]
+        vkT_ps, qT_ps, den_ps, hs_ps, aT_ps, woT_ps, out_ps = {}, {}, {}, {}, {}, {}, {}
+
+        def transpose_vk(u):
+            vkT_ps[u] = psum.tile([P, PACK, PACK, PH], BF16, tag="tin", bufs=3, name="vkT_ps")
             for i in range(PACK):
-                nc.tensor.transpose(vkT_ps[:, :, i, :], vk_sb[u][:, i, :], ident[:])
-            nc.scalar.copy(out=vkT[u][:], in_=vkT_ps[:])
-            for j in range(TOKEN_TILES):
-                qT_ps = psum.tile([P, PACK, PER, PH], BF16, tag="tin", bufs=3)
-                for jj in range(PER):
-                    nc.tensor.transpose(qT_ps[:, :, jj, :], q_sb[u][:, TOKEN_TILES * jj + j, :], ident[:])
-                nc.scalar.copy(out=qT[u][:, j], in_=qT_ps[:])
+                nc.tensor.transpose(vkT_ps[u][:, :, i, :], vk_sb[u][:, i, :], ident[:])
+
+        def copy_vk(u):
+            nc.scalar.copy(out=vkT[u][:], in_=vkT_ps[u][:])
+
+        def transpose_q(u, j):
+            qT_ps[u, j] = psum.tile([P, PACK, PER, PH], BF16, tag="tin", bufs=3, name="qT_ps")
+            for jj in range(PER):
+                nc.tensor.transpose(qT_ps[u, j][:, :, jj, :], q_sb[u][:, TOKEN_TILES * jj + j, :], ident[:])
+
+        def copy_q(u, j):
+            nc.scalar.copy(out=qT[u][:, j], in_=qT_ps[u, j][:])
+
+        def queries(u, j, h):
+            return qT[u][:, j, h].rearrange("d jj p -> d (jj p)")
+
+        def den_matmuls(u, j):
+            den_ps[u, j] = psum.tile([P, PACK], F32, tag="den", bufs=1, name="den_ps")
+            for h in range(PACK):
+                bh = PACK * u + h
+                nc.tensor.matmul(out=den_ps[u, j][:, h : h + 1], lhsT=queries(u, j, h), rhs=ksT[:, bh : bh + 1], start=True, stop=True)
+
+        def den_guard(u, j):
+            nc.scalar.activation(out=den[u][:, j], in_=den_ps[u, j][:], func=COPY, bias=EPS)
+
+        def den_recip(u, j):
+            nc.vector.reciprocal(out=recip[u][:, j], in_=den[u][:, j].unsqueeze(1).to_broadcast([P, HALVES, PACK]))
+
+        def hs_matmuls(u, j):
+            hs_ps[u, j] = psum.tile([P, HALVES, PACK, HALVES, PH], F32, tag="hs", bufs=3, name="hs_ps")
+            for h in range(PACK):
+                nc.tensor.matmul(
+                    out=hs_ps[u, j][:, :, h, :, :],
+                    lhsT=queries(u, j, h),
+                    rhs=vkT[u][:, h].rearrange("d (w e) m -> d w e m", w=HALVES),
+                    start=True,
+                    stop=True,
+                )
+
+        def normalise(u, j):
+            nc.vector.tensor_tensor(
+                out=a_sb[u][:, j].rearrange("p w (h m e) -> p (w h) m e", h=PACK, e=HALVES),
+                in0=hs_ps[u, j][:].rearrange("p w h e m -> p (w h) m e"),
+                in1=recip[u][:, j].rearrange("p w h -> p (w h)").unsqueeze(2).unsqueeze(3).to_broadcast([P, HALVES * PACK, PH, HALVES]),
+                op=MULT,
+            )
+
+        def transpose_a(u, j):
+            aT_ps[u, j] = psum.tile([P, HALVES, P], F32, tag="aT", bufs=1, name="aT_ps")
+            for w in range(HALVES):
+                nc.tensor.transpose(aT_ps[u, j][:, w, :], a_sb[u][:, j, w, :].bitcast(F32), sort_f32[:])
+
+        def copy_a(u, j):
+            nc.scalar.copy(
+                out=a_grouped[u][:, j].rearrange("n q t -> n (q t)").bitcast(F32).rearrange("n (q w) -> n q w", w=HALVES),
+                in_=aT_ps[u, j][:].rearrange("n w q -> n q w"),
+            )
+
+        def quantise_a(u, j):
+            nc.vector.quantize_mx(
+                out=a_codes[u][:, j, :].bitcast(FP8X4),
+                scales=a_scales[u][:, j, :],
+                in_=a_grouped[u][:, j, :, :].rearrange("n q t -> n (q t)"),
+            )
+
+        wo_words = wo_sb[:].bitcast(F32)
+
+        def transpose_wo(g):
+            woT_ps[g] = psum.tile([P, HALVES, C_TILES, P], F32, tag="tin", bufs=3, name="woT_ps")
+            for w in range(HALVES):
+                for ct in range(C_TILES):
+                    every_second = wo_words[:, ct, HALVES * P * g + w : HALVES * P * (g + 1) : HALVES]
+                    nc.tensor.transpose(woT_ps[g][:, w, ct, :], every_second, ident_f32[:])
+
+        def copy_wo(g):
+            nc.scalar.copy(
+                out=w_grouped[:, g].rearrange("n c t -> n (c t)").bitcast(F32).rearrange("n (p ct w) -> n p ct w", ct=C_TILES, w=HALVES),
+                in_=woT_ps[g][:].rearrange("n w ct p -> n p ct w"),
+            )
 
         def quantise_wo():
-            wo_words = wo_sb[:].bitcast(F32)
-            for g in range(GROUPS):
-                woT_ps = psum.tile([P, HALVES, C_TILES, P], F32, tag="tin", bufs=3)
-                for w in range(HALVES):
-                    for ct in range(C_TILES):
-                        every_second = wo_words[:, ct, HALVES * P * g + w : HALVES * P * (g + 1) : HALVES]
-                        nc.tensor.transpose(woT_ps[:, w, ct, :], every_second, ident_f32[:])
-                nc.vector.tensor_copy(
-                    out=w_grouped[:, g].rearrange("n c t -> n (c t)").bitcast(F32).rearrange("n (p ct w) -> n p ct w", ct=C_TILES, w=HALVES),
-                    in_=woT_ps[:].rearrange("n w ct p -> n p ct w"),
-                )
             nc.vector.quantize_mx(
                 out=w_codes[:].rearrange("n g c -> n (g c)").bitcast(FP8X4),
                 scales=w_scales[:].rearrange("n g c -> n (g c)"),
                 in_=w_grouped[:].rearrange("n g c t -> n (g c t)"),
             )
 
-        recip = [keep.tile([P, TOKEN_TILES, HALVES, PACK], F32, name="recip%d" % u) for u in range(UNITS)]
-
-        def denominators(u):
-            den_ps = psum.tile([P, TOKEN_TILES, PACK], F32, tag="den", bufs=1)
-            for j in range(TOKEN_TILES):
-                for h in range(PACK):
-                    bh = PACK * u + h
-                    nc.tensor.matmul(
-                        out=den_ps[:, j, h : h + 1],
-                        lhsT=qT[u][:, j, h].rearrange("d jj p -> d (jj p)"),
-                        rhs=ksT[:, bh : bh + 1],
-                        start=True,
-                        stop=True,
-                    )
-            den = keep.tile([P, TOKEN_TILES, PACK], F32, name="den%d" % u)
-            nc.vector.tensor_scalar_add(out=den[:], in0=den_ps[:], scalar1=EPS)
-            nc.vector.reciprocal(out=recip[u][:], in_=den[:].unsqueeze(2).to_broadcast([P, TOKEN_TILES, HALVES, PACK]))
-
-        def read_out(u):
-            for j in range(TOKEN_TILES):
-                hs_ps = psum.tile([P, HALVES, PACK, HALVES, PH], F32, tag="hs")
-                for h in range(PACK):
-                    nc.tensor.matmul(
-                        out=hs_ps[:, :, h, :, :],
-                        lhsT=qT[u][:, j, h].rearrange("d jj p -> d (jj p)"),
-                        rhs=vkT[u][:, h].rearrange("d (w e) m -> d w e m", w=HALVES),
-                        start=True,
-                        stop=True,
-                    )
-                nc.vector.tensor_tensor(
-                    out=a_sb[u][:, j].rearrange("p w (h m e) -> p (w h) m e", h=PACK, e=HALVES),
-                    in0=hs_ps[:].rearrange("p w h e m -> p (w h) m e"),
-                    in1=recip[u][:, j].rearrange("p w h -> p (w h)").unsqueeze(2).unsqueeze(3).to_broadcast([P, HALVES * PACK, PH, HALVES]),
-                    op=MULT,
-                )
-
-        def quantise_a(u):
-            for j in range(TOKEN_TILES):
-                aT_ps = psum.tile([P, HALVES, P], F32, tag="aT")
-                for w in range(HALVES):
-                    nc.tensor.transpose(aT_ps[:, w, :], a_sb[u][:, j, w, :].bitcast(F32), sort_f32[:])
-                nc.scalar.copy(
-                    out=a_grouped[u][:, j].rearrange("n q t -> n (q t)").bitcast(F32).rearrange("n (q w) -> n q w", w=HALVES),
-                    in_=aT_ps[:].rearrange("n w q -> n q w"),
-                )
-                nc.vector.quantize_mx(
-                    out=a_codes[u][:, j, :].bitcast(FP8X4),
-                    scales=a_scales[u][:, j, :],
-                    in_=a_grouped[u][:, j, :, :].rearrange("n q t -> n (q t)"),
-                )
-
         def project(b, j):
-            out_ps = psum.tile([P, C], F32, tag="hs")
+            out_ps[b, j] = psum.tile([P, C], F32, tag="hs", bufs=3, name="out_ps")
             for g in range(GROUPS):
                 u = GROUPS * b + g
                 nc.tensor.matmul_mx(
-                    out=out_ps[:],
+                    out=out_ps[b, j][:],
                     lhsT=a_codes[u][:, j, :].bitcast(FP8X4),
                     lhsT_scale=a_scales[u][:, j, :],
                     rhs=w_codes[:, g, :].bitcast(FP8X4),
@@ -169,20 +184,48 @@ def tile_lineartransformerblock_pc_s_kernel(tc, q_feat, vk, k_sum, Wo, bo, out):
                     start=(g == 0),
                     stop=(g == GROUPS - 1),
                 )
+
+        def finish(b, j):
             out_sb = keep.tile([P, C], F32, name="out_sb%d%d" % (b, j))
-            nc.vector.tensor_tensor(out=out_sb[:], in0=out_ps[:], in1=bias[:], op=ADD)
+            nc.vector.tensor_tensor(out=out_sb[:], in0=out_ps[b, j][:], in1=bias[:], op=ADD)
             nc.sync.dma_start(out=out[b].rearrange("(q j) c -> q j c", j=TOKEN_TILES)[:, j, :], in_=out_sb[:])
 
-        for step in range(UNITS + 2):
-            if step < UNITS:
-                transpose_inputs(step)
-                denominators(step)
-            if 1 <= step <= UNITS:
-                read_out(step - 1)
-            if step == 1:
-                quantise_wo()
-            if step >= 2:
-                quantise_a(step - 2)
-        for b in range(B):
-            for j in range(TOKEN_TILES):
-                project(b, j)
+        halves = [(u, j) for u in range(UNITS) for j in range(TOKEN_TILES)]
+
+        def at(stage, n):
+            if 0 <= n < len(halves):
+                stage(*halves[n])
+
+        with tc.manual_schedule():
+            transpose_vk(0)
+            transpose_q(0, 0)
+            copy_vk(0)
+            for n in range(len(halves) + 5):
+                at(copy_q, n)
+                at(den_guard, n - 1)
+                at(copy_a, n - 3)
+                if n % 2 == 1 and n // 2 + 1 < UNITS:
+                    copy_vk(n // 2 + 1)
+                if n == 3:
+                    copy_wo(0)
+                if n == 5:
+                    copy_wo(1)
+                at(hs_matmuls, n - 1)
+                at(transpose_q, n + 1)
+                if n % 2 == 0 and n // 2 + 1 < UNITS:
+                    transpose_vk(n // 2 + 1)
+                at(den_matmuls, n)
+                at(transpose_a, n - 2)
+                if n == 2:
+                    transpose_wo(0)
+                if n == 4:
+                    transpose_wo(1)
+                at(den_recip, n - 1)
+                at(quantise_a, n - 3)
+                at(normalise, n - 1)
+                if n == 5:
+                    quantise_wo()
+                k = n - 5
+                if 0 <= k < len(halves) and halves[k][0] % GROUPS == 1:
+                    project(halves[k][0] // GROUPS, halves[k][1])
+                    finish(halves[k][0] // GROUPS, halves[k][1])

@@ -53,6 +53,12 @@ def tile_lineartransformerblock_pc_s_kernel(tc, q_feat, vk, k_sum, Wo, bo, out):
             load_unit(u)
         nc.sync.dma_start(out=bias[:], in_=bo.partition_broadcast(P))
 
+        zeros = keep.tile([P, P], F32)
+        nc.vector.memset(zeros[:], 0.0)
+        idle_ps = psum.tile([P, P], F32, tag="aT", bufs=1, name="idle_ps")
+        for repeat in range(3):
+            nc.tensor.matmul(out=idle_ps[:], lhsT=zeros[:], rhs=zeros[:], start=True, stop=True)
+
         ident = keep.tile([P, P], BF16)
         make_identity(nc, ident[:])
         ident_f32 = keep.tile([P, P], F32)
@@ -87,7 +93,7 @@ def tile_lineartransformerblock_pc_s_kernel(tc, q_feat, vk, k_sum, Wo, bo, out):
                 nc.tensor.transpose(vkT_ps[u][:, :, i, :], vk_sb[u][:, i, :], ident[:])
 
         def copy_vk(u):
-            nc.scalar.copy(out=vkT[u][:], in_=vkT_ps[u][:])
+            nc.vector.tensor_copy(out=vkT[u][:], in_=vkT_ps[u][:])
 
         def transpose_q(u, j):
             qT_ps[u, j] = psum.tile([P, PACK, PER, PH], BF16, tag="tin", bufs=3, name="qT_ps")
@@ -95,7 +101,10 @@ def tile_lineartransformerblock_pc_s_kernel(tc, q_feat, vk, k_sum, Wo, bo, out):
                 nc.tensor.transpose(qT_ps[u, j][:, :, jj, :], q_sb[u][:, TOKEN_TILES * jj + j, :], ident[:])
 
         def copy_q(u, j):
-            nc.scalar.copy(out=qT[u][:, j], in_=qT_ps[u, j][:])
+            if (u, j) == (0, 0):
+                nc.vector.tensor_copy(out=qT[u][:, j], in_=qT_ps[u, j][:])
+            else:
+                nc.scalar.copy(out=qT[u][:, j], in_=qT_ps[u, j][:])
 
         def queries(u, j, h):
             return qT[u][:, j, h].rearrange("d jj p -> d (jj p)")
@@ -124,6 +133,15 @@ def tile_lineartransformerblock_pc_s_kernel(tc, q_feat, vk, k_sum, Wo, bo, out):
                 )
 
         def normalise(u, j):
+            if (u, j) == (UNITS - 1, TOKEN_TILES - 1):
+                for h in range(PACK):
+                    nc.scalar.activation(
+                        out=a_sb[u][:, j].rearrange("p w (h m e) -> p w h m e", h=PACK, e=HALVES)[:, :, h],
+                        in_=hs_ps[u, j][:, :, h].rearrange("p w e m -> p w m e"),
+                        func=COPY,
+                        scale=recip[u][:, j, 0, h : h + 1],
+                    )
+                return
             nc.vector.tensor_tensor(
                 out=a_sb[u][:, j].rearrange("p w (h m e) -> p (w h) m e", h=PACK, e=HALVES),
                 in0=hs_ps[u, j][:].rearrange("p w h e m -> p (w h) m e"),
@@ -200,15 +218,15 @@ def tile_lineartransformerblock_pc_s_kernel(tc, q_feat, vk, k_sum, Wo, bo, out):
             transpose_vk(0)
             transpose_q(0, 0)
             copy_vk(0)
-            for n in range(len(halves) + 5):
+            for n in range(len(halves) + 6):
                 at(copy_q, n)
                 at(den_guard, n - 1)
                 at(copy_a, n - 3)
                 if n % 2 == 1 and n // 2 + 1 < UNITS:
                     copy_vk(n // 2 + 1)
-                if n == 3:
+                if n == 6:
                     copy_wo(0)
-                if n == 5:
+                if n == 7:
                     copy_wo(1)
                 at(hs_matmuls, n - 1)
                 at(transpose_q, n + 1)
@@ -216,16 +234,21 @@ def tile_lineartransformerblock_pc_s_kernel(tc, q_feat, vk, k_sum, Wo, bo, out):
                     transpose_vk(n // 2 + 1)
                 at(den_matmuls, n)
                 at(transpose_a, n - 2)
-                if n == 2:
+                if n == 5:
                     transpose_wo(0)
-                if n == 4:
+                if n == 6:
                     transpose_wo(1)
                 at(den_recip, n - 1)
                 at(quantise_a, n - 3)
                 at(normalise, n - 1)
-                if n == 5:
+                if n == 8:
                     quantise_wo()
-                k = n - 5
+                k = n - 6
                 if 0 <= k < len(halves) and halves[k][0] % GROUPS == 1:
                     project(halves[k][0] // GROUPS, halves[k][1])
+                k = n - 7
+                if 0 <= k < len(halves) and halves[k][0] % GROUPS == 1 and halves[k][0] < GROUPS:
+                    finish(halves[k][0] // GROUPS, halves[k][1])
+                k = n - 6
+                if 0 <= k < len(halves) and halves[k][0] % GROUPS == 1 and halves[k][0] >= GROUPS:
                     finish(halves[k][0] // GROUPS, halves[k][1])

@@ -55,7 +55,7 @@ def tile_lineartransformerblock_pc_s_kernel(tc, q_feat, vk, k_sum, Wo, bo, out):
 
         zeros = keep.tile([P, P], F32)
         nc.vector.memset(zeros[:], 0.0)
-        idle_ps = psum.tile([P, P], F32, tag="aT", bufs=1, name="idle_ps")
+        idle_ps = psum.tile([P, P], F32, tag="step", bufs=2, name="idle_ps")
         for repeat in range(3):
             nc.tensor.matmul(out=idle_ps[:], lhsT=zeros[:], rhs=zeros[:], start=True, stop=True)
 
@@ -68,7 +68,7 @@ def tile_lineartransformerblock_pc_s_kernel(tc, q_feat, vk, k_sum, Wo, bo, out):
             out=sort_f32[:].rearrange("k (p jj) -> k p jj", jj=PER), in_=ident_f32[:].rearrange("k (jj p) -> k p jj", jj=PER)
         )
 
-        ksT_ps = psum.tile([P, PACK * P], BF16, tag="tin", bufs=3)
+        ksT_ps = psum.tile([P, PACK * P], BF16, tag="tin", bufs=4)
         nc.tensor.transpose(ksT_ps[:, 0:P], ks_rows[:], ident[:])
         ksT = keep.tile([P, B * H], BF16)
         nc.scalar.copy(out=ksT[:], in_=ksT_ps[:, 0 : B * H])
@@ -88,7 +88,7 @@ def tile_lineartransformerblock_pc_s_kernel(tc, q_feat, vk, k_sum, Wo, bo, out):
         vkT_ps, qT_ps, den_ps, hs_ps, aT_ps, woT_ps, out_ps = {}, {}, {}, {}, {}, {}, {}
 
         def transpose_vk(u):
-            vkT_ps[u] = psum.tile([P, PACK, PACK, PH], BF16, tag="tin", bufs=3, name="vkT_ps")
+            vkT_ps[u] = psum.tile([P, PACK, PACK, PH], BF16, tag="tin", bufs=4, name="vkT_ps")
             for i in range(PACK):
                 nc.tensor.transpose(vkT_ps[u][:, :, i, :], vk_sb[u][:, i, :], ident[:])
 
@@ -96,12 +96,12 @@ def tile_lineartransformerblock_pc_s_kernel(tc, q_feat, vk, k_sum, Wo, bo, out):
             nc.vector.tensor_copy(out=vkT[u][:], in_=vkT_ps[u][:])
 
         def transpose_q(u, j):
-            qT_ps[u, j] = psum.tile([P, PACK, PER, PH], BF16, tag="tin", bufs=3, name="qT_ps")
+            qT_ps[u, j] = psum.tile([P, PACK, PER, PH], BF16, tag="tin", bufs=4, name="qT_ps")
             for jj in range(PER):
                 nc.tensor.transpose(qT_ps[u, j][:, :, jj, :], q_sb[u][:, TOKEN_TILES * jj + j, :], ident[:])
 
         def copy_q(u, j):
-            if (u, j) == (0, 0):
+            if u == 0:
                 nc.vector.tensor_copy(out=qT[u][:, j], in_=qT_ps[u, j][:])
             else:
                 nc.scalar.copy(out=qT[u][:, j], in_=qT_ps[u, j][:])
@@ -109,20 +109,27 @@ def tile_lineartransformerblock_pc_s_kernel(tc, q_feat, vk, k_sum, Wo, bo, out):
         def queries(u, j, h):
             return qT[u][:, j, h].rearrange("d jj p -> d (jj p)")
 
+        banks = {}
+
+        def step_bank(n):
+            if n not in banks:
+                banks[n] = psum.tile([P, HALVES * P + PACK], F32, tag="step", bufs=2, name="step_ps")
+            return banks[n]
+
         def den_matmuls(u, j):
-            den_ps[u, j] = psum.tile([P, PACK], F32, tag="den", bufs=1, name="den_ps")
+            den_ps[u, j] = step_bank(TOKEN_TILES * u + j)[:, HALVES * P : HALVES * P + PACK]
             for h in range(PACK):
                 bh = PACK * u + h
                 nc.tensor.matmul(out=den_ps[u, j][:, h : h + 1], lhsT=queries(u, j, h), rhs=ksT[:, bh : bh + 1], start=True, stop=True)
 
         def den_guard(u, j):
-            nc.scalar.activation(out=den[u][:, j], in_=den_ps[u, j][:], func=COPY, bias=EPS)
+            nc.scalar.activation(out=den[u][:, j], in_=den_ps[u, j], func=COPY, bias=EPS)
 
         def den_recip(u, j):
             nc.vector.reciprocal(out=recip[u][:, j], in_=den[u][:, j].unsqueeze(1).to_broadcast([P, HALVES, PACK]))
 
         def hs_matmuls(u, j):
-            hs_ps[u, j] = psum.tile([P, HALVES, PACK, HALVES, PH], F32, tag="hs", bufs=3, name="hs_ps")
+            hs_ps[u, j] = psum.tile([P, HALVES, PACK, HALVES, PH], F32, tag="hs", bufs=2, name="hs_ps")
             for h in range(PACK):
                 nc.tensor.matmul(
                     out=hs_ps[u, j][:, :, h, :, :],
@@ -150,14 +157,14 @@ def tile_lineartransformerblock_pc_s_kernel(tc, q_feat, vk, k_sum, Wo, bo, out):
             )
 
         def transpose_a(u, j):
-            aT_ps[u, j] = psum.tile([P, HALVES, P], F32, tag="aT", bufs=1, name="aT_ps")
+            aT_ps[u, j] = step_bank(TOKEN_TILES * u + j + 2)[:, 0 : HALVES * P].rearrange("n (w q) -> n w q", w=HALVES)
             for w in range(HALVES):
                 nc.tensor.transpose(aT_ps[u, j][:, w, :], a_sb[u][:, j, w, :].bitcast(F32), sort_f32[:])
 
         def copy_a(u, j):
             nc.scalar.copy(
                 out=a_grouped[u][:, j].rearrange("n q t -> n (q t)").bitcast(F32).rearrange("n (q w) -> n q w", w=HALVES),
-                in_=aT_ps[u, j][:].rearrange("n w q -> n q w"),
+                in_=aT_ps[u, j].rearrange("n w q -> n q w"),
             )
 
         def quantise_a(u, j):
@@ -170,7 +177,7 @@ def tile_lineartransformerblock_pc_s_kernel(tc, q_feat, vk, k_sum, Wo, bo, out):
         wo_words = wo_sb[:].bitcast(F32)
 
         def transpose_wo(g):
-            woT_ps[g] = psum.tile([P, HALVES, C_TILES, P], F32, tag="tin", bufs=3, name="woT_ps")
+            woT_ps[g] = psum.tile([P, HALVES, C_TILES, P], F32, tag="tin", bufs=4, name="woT_ps")
             for w in range(HALVES):
                 for ct in range(C_TILES):
                     every_second = wo_words[:, ct, HALVES * P * g + w : HALVES * P * (g + 1) : HALVES]
@@ -190,7 +197,7 @@ def tile_lineartransformerblock_pc_s_kernel(tc, q_feat, vk, k_sum, Wo, bo, out):
             )
 
         def project(b, j):
-            out_ps[b, j] = psum.tile([P, C], F32, tag="hs", bufs=3, name="out_ps")
+            out_ps[b, j] = psum.tile([P, C], F32, tag="tin", bufs=4, name="out_ps")
             for g in range(GROUPS):
                 u = GROUPS * b + g
                 nc.tensor.matmul_mx(
@@ -218,7 +225,7 @@ def tile_lineartransformerblock_pc_s_kernel(tc, q_feat, vk, k_sum, Wo, bo, out):
             transpose_vk(0)
             transpose_q(0, 0)
             copy_vk(0)
-            for n in range(len(halves) + 6):
+            for n in range(len(halves) + 2):
                 at(copy_q, n)
                 at(den_guard, n - 1)
                 at(copy_a, n - 3)
@@ -243,12 +250,13 @@ def tile_lineartransformerblock_pc_s_kernel(tc, q_feat, vk, k_sum, Wo, bo, out):
                 at(normalise, n - 1)
                 if n == 8:
                     quantise_wo()
-                k = n - 6
-                if 0 <= k < len(halves) and halves[k][0] % GROUPS == 1:
-                    project(halves[k][0] // GROUPS, halves[k][1])
-                k = n - 7
-                if 0 <= k < len(halves) and halves[k][0] % GROUPS == 1 and halves[k][0] < GROUPS:
-                    finish(halves[k][0] // GROUPS, halves[k][1])
-                k = n - 6
-                if 0 <= k < len(halves) and halves[k][0] % GROUPS == 1 and halves[k][0] >= GROUPS:
-                    finish(halves[k][0] // GROUPS, halves[k][1])
+            copy_a(*halves[-1])
+            project(0, 0)
+            project(0, 1)
+            finish(0, 0)
+            quantise_a(*halves[-1])
+            finish(0, 1)
+            project(1, 0)
+            project(1, 1)
+            finish(1, 0)
+            finish(1, 1)

@@ -30,8 +30,8 @@ def tile_lineartransformerblock_pc_s_kernel(tc, q_feat, vk, k_sum, Wo, bo, out):
     nc = tc.nc
     with tc.tile_pool(name="keep", bufs=1) as keep, tc.psum_pool(name="psum", bufs=1) as psum:
         ks_rows = keep.tile([P, D], BF16)
-        nc.vector.memset(ks_rows[:], 0.0)
-        nc.sync.dma_start(out=ks_rows[0 : B * H, :], in_=k_sum.rearrange("b h d -> (b h) d"))
+        nc.gpsimd.memset(ks_rows[:], 0.0)
+        nc.scalar.dma_start(out=ks_rows[0 : B * H, :], in_=k_sum.rearrange("b h d -> (b h) d"))
 
         vk_sb = [keep.tile([P, PACK, D], BF16, name="vk_sb%d" % u) for u in range(UNITS)]
         q_sb = [keep.tile([P, RUN, D], BF16, name="q_sb%d" % u) for u in range(UNITS)]

@@ -21,6 +21,7 @@ RUN = S // PH
 TOKEN_TILES = S // P
 PER = RUN // TOKEN_TILES
 C_TILES = C // P
+BANKS = 8
 HALVES = 2
 
 FLOPS = 2 * B * H * S * D * D + 2 * B * H * S * D + 2 * B * S * H * D * C
@@ -55,7 +56,7 @@ def tile_lineartransformerblock_pc_s_kernel(tc, q_feat, vk, k_sum, Wo, bo, out):
 
         zeros = keep.tile([P, P], F32)
         nc.vector.memset(zeros[:], 0.0)
-        idle_ps = psum.tile([P, P], F32, tag="step", bufs=2, name="idle_ps")
+        idle_ps = psum.tile([P, P], F32, tag="bank", bufs=BANKS, name="idle_ps")
         for repeat in range(3):
             nc.tensor.matmul(out=idle_ps[:], lhsT=zeros[:], rhs=zeros[:], start=True, stop=True)
 
@@ -68,7 +69,7 @@ def tile_lineartransformerblock_pc_s_kernel(tc, q_feat, vk, k_sum, Wo, bo, out):
             out=sort_f32[:].rearrange("k (p jj) -> k p jj", jj=PER), in_=ident_f32[:].rearrange("k (jj p) -> k p jj", jj=PER)
         )
 
-        ksT_ps = psum.tile([P, PACK * P], BF16, tag="tin", bufs=4)
+        ksT_ps = psum.tile([P, PACK * P], BF16, tag="bank", bufs=BANKS)
         nc.tensor.transpose(ksT_ps[:, 0:P], ks_rows[:], ident[:])
         ksT = keep.tile([P, B * H], BF16)
         nc.scalar.copy(out=ksT[:], in_=ksT_ps[:, 0 : B * H])
@@ -88,48 +89,45 @@ def tile_lineartransformerblock_pc_s_kernel(tc, q_feat, vk, k_sum, Wo, bo, out):
         vkT_ps, qT_ps, den_ps, hs_ps, aT_ps, woT_ps, out_ps = {}, {}, {}, {}, {}, {}, {}
 
         def transpose_vk(u):
-            vkT_ps[u] = psum.tile([P, PACK, PACK, PH], BF16, tag="tin", bufs=4, name="vkT_ps")
+            vkT_ps[u] = psum.tile([P, PACK, PACK, PH], BF16, tag="bank", bufs=BANKS, name="vkT_ps")
             for i in range(PACK):
                 nc.tensor.transpose(vkT_ps[u][:, :, i, :], vk_sb[u][:, i, :], ident[:])
 
-        def copy_vk(u):
-            nc.vector.tensor_copy(out=vkT[u][:], in_=vkT_ps[u][:])
+        def copy(engine, out, in_):
+            if engine is nc.scalar:
+                nc.scalar.copy(out=out, in_=in_)
+            else:
+                nc.vector.tensor_copy(out=out, in_=in_)
+
+        def copy_vk(u, engine):
+            copy(engine, vkT[u][:], vkT_ps[u][:])
 
         def transpose_q(u, j):
-            qT_ps[u, j] = psum.tile([P, PACK, PER, PH], BF16, tag="tin", bufs=4, name="qT_ps")
+            qT_ps[u, j] = psum.tile([P, PACK, PER, PH], BF16, tag="bank", bufs=BANKS, name="qT_ps")
             for jj in range(PER):
                 nc.tensor.transpose(qT_ps[u, j][:, :, jj, :], q_sb[u][:, TOKEN_TILES * jj + j, :], ident[:])
 
-        def copy_q(u, j):
-            if u == 0:
-                nc.vector.tensor_copy(out=qT[u][:, j], in_=qT_ps[u, j][:])
-            else:
-                nc.scalar.copy(out=qT[u][:, j], in_=qT_ps[u, j][:])
+        def copy_q(u, j, engine):
+            copy(engine, qT[u][:, j], qT_ps[u, j][:])
 
         def queries(u, j, h):
             return qT[u][:, j, h].rearrange("d jj p -> d (jj p)")
 
-        banks = {}
-
-        def step_bank(n):
-            if n not in banks:
-                banks[n] = psum.tile([P, HALVES * P + PACK], F32, tag="step", bufs=2, name="step_ps")
-            return banks[n]
-
         def den_matmuls(u, j):
-            den_ps[u, j] = step_bank(TOKEN_TILES * u + j)[:, HALVES * P : HALVES * P + PACK]
+            if j == 0:
+                den_ps[u] = psum.tile([P, TOKEN_TILES, PACK], F32, tag="bank", bufs=BANKS, name="den_ps")
             for h in range(PACK):
                 bh = PACK * u + h
-                nc.tensor.matmul(out=den_ps[u, j][:, h : h + 1], lhsT=queries(u, j, h), rhs=ksT[:, bh : bh + 1], start=True, stop=True)
+                nc.tensor.matmul(out=den_ps[u][:, j, h : h + 1], lhsT=queries(u, j, h), rhs=ksT[:, bh : bh + 1], start=True, stop=True)
 
-        def den_guard(u, j):
-            nc.scalar.activation(out=den[u][:, j], in_=den_ps[u, j], func=COPY, bias=EPS)
+        def den_guard(u):
+            nc.scalar.activation(out=den[u][:], in_=den_ps[u][:], func=COPY, bias=EPS)
 
-        def den_recip(u, j):
-            nc.vector.reciprocal(out=recip[u][:, j], in_=den[u][:, j].unsqueeze(1).to_broadcast([P, HALVES, PACK]))
+        def den_recip(u):
+            nc.vector.reciprocal(out=recip[u][:], in_=den[u][:].unsqueeze(2).to_broadcast([P, TOKEN_TILES, HALVES, PACK]))
 
         def hs_matmuls(u, j):
-            hs_ps[u, j] = psum.tile([P, HALVES, PACK, HALVES, PH], F32, tag="hs", bufs=2, name="hs_ps")
+            hs_ps[u, j] = psum.tile([P, HALVES, PACK, HALVES, PH], F32, tag="bank", bufs=BANKS, name="hs_ps")
             for h in range(PACK):
                 nc.tensor.matmul(
                     out=hs_ps[u, j][:, :, h, :, :],
@@ -139,8 +137,8 @@ def tile_lineartransformerblock_pc_s_kernel(tc, q_feat, vk, k_sum, Wo, bo, out):
                     stop=True,
                 )
 
-        def normalise(u, j):
-            if (u, j) == (UNITS - 1, TOKEN_TILES - 1):
+        def normalise(u, j, engine):
+            if engine is nc.scalar:
                 for h in range(PACK):
                     nc.scalar.activation(
                         out=a_sb[u][:, j].rearrange("p w (h m e) -> p w h m e", h=PACK, e=HALVES)[:, :, h],
@@ -157,14 +155,15 @@ def tile_lineartransformerblock_pc_s_kernel(tc, q_feat, vk, k_sum, Wo, bo, out):
             )
 
         def transpose_a(u, j):
-            aT_ps[u, j] = step_bank(TOKEN_TILES * u + j + 2)[:, 0 : HALVES * P].rearrange("n (w q) -> n w q", w=HALVES)
+            aT_ps[u, j] = psum.tile([P, HALVES, P], F32, tag="bank", bufs=BANKS, name="aT_ps")
             for w in range(HALVES):
                 nc.tensor.transpose(aT_ps[u, j][:, w, :], a_sb[u][:, j, w, :].bitcast(F32), sort_f32[:])
 
-        def copy_a(u, j):
-            nc.scalar.copy(
-                out=a_grouped[u][:, j].rearrange("n q t -> n (q t)").bitcast(F32).rearrange("n (q w) -> n q w", w=HALVES),
-                in_=aT_ps[u, j].rearrange("n w q -> n q w"),
+        def copy_a(u, j, engine):
+            copy(
+                engine,
+                a_grouped[u][:, j].rearrange("n q t -> n (q t)").bitcast(F32).rearrange("n (q w) -> n q w", w=HALVES),
+                aT_ps[u, j][:].rearrange("n w q -> n q w"),
             )
 
         def quantise_a(u, j):
@@ -177,7 +176,7 @@ def tile_lineartransformerblock_pc_s_kernel(tc, q_feat, vk, k_sum, Wo, bo, out):
         wo_words = wo_sb[:].bitcast(F32)
 
         def transpose_wo(g):
-            woT_ps[g] = psum.tile([P, HALVES, C_TILES, P], F32, tag="tin", bufs=4, name="woT_ps")
+            woT_ps[g] = psum.tile([P, HALVES, C_TILES, P], F32, tag="bank", bufs=BANKS, name="woT_ps")
             for w in range(HALVES):
                 for ct in range(C_TILES):
                     every_second = wo_words[:, ct, HALVES * P * g + w : HALVES * P * (g + 1) : HALVES]
@@ -189,15 +188,13 @@ def tile_lineartransformerblock_pc_s_kernel(tc, q_feat, vk, k_sum, Wo, bo, out):
                 in_=woT_ps[g][:].rearrange("n w ct p -> n p ct w"),
             )
 
-        def quantise_wo():
+        def quantise_wo(g):
             nc.vector.quantize_mx(
-                out=w_codes[:].rearrange("n g c -> n (g c)").bitcast(FP8X4),
-                scales=w_scales[:].rearrange("n g c -> n (g c)"),
-                in_=w_grouped[:].rearrange("n g c t -> n (g c t)"),
+                out=w_codes[:, g].bitcast(FP8X4), scales=w_scales[:, g], in_=w_grouped[:, g].rearrange("n c t -> n (c t)")
             )
 
         def project(b, j):
-            out_ps[b, j] = psum.tile([P, C], F32, tag="tin", bufs=4, name="out_ps")
+            out_ps[b, j] = psum.tile([P, C], F32, tag="bank", bufs=BANKS, name="out_ps")
             for g in range(GROUPS):
                 u = GROUPS * b + g
                 nc.tensor.matmul_mx(
@@ -215,48 +212,62 @@ def tile_lineartransformerblock_pc_s_kernel(tc, q_feat, vk, k_sum, Wo, bo, out):
             nc.vector.tensor_tensor(out=out_sb[:], in0=out_ps[b, j][:], in1=bias[:], op=ADD)
             nc.sync.dma_start(out=out[b].rearrange("(q j) c -> q j c", j=TOKEN_TILES)[:, j, :], in_=out_sb[:])
 
-        halves = [(u, j) for u in range(UNITS) for j in range(TOKEN_TILES)]
-
-        def at(stage, n):
-            if 0 <= n < len(halves):
-                stage(*halves[n])
-
+        V, A = nc.vector, nc.scalar
         with tc.manual_schedule():
-            transpose_vk(0)
-            transpose_q(0, 0)
-            copy_vk(0)
-            for n in range(len(halves) + 2):
-                at(copy_q, n)
-                at(den_guard, n - 1)
-                at(copy_a, n - 3)
-                if n % 2 == 1 and n // 2 + 1 < UNITS:
-                    copy_vk(n // 2 + 1)
-                if n == 6:
-                    copy_wo(0)
-                if n == 7:
-                    copy_wo(1)
-                at(hs_matmuls, n - 1)
-                at(transpose_q, n + 1)
-                if n % 2 == 0 and n // 2 + 1 < UNITS:
-                    transpose_vk(n // 2 + 1)
-                at(den_matmuls, n)
-                at(transpose_a, n - 2)
-                if n == 5:
-                    transpose_wo(0)
-                if n == 6:
-                    transpose_wo(1)
-                at(den_recip, n - 1)
-                at(quantise_a, n - 3)
-                at(normalise, n - 1)
-                if n == 8:
-                    quantise_wo()
-            copy_a(*halves[-1])
-            project(0, 0)
-            project(0, 1)
-            finish(0, 0)
-            quantise_a(*halves[-1])
-            finish(0, 1)
-            project(1, 0)
-            project(1, 1)
-            finish(1, 0)
-            finish(1, 1)
+            for u, engines in ((0, (A, V, A)), (1, (V, A, V))):
+                transpose_vk(u)
+                copy_vk(u, engines[0])
+                for j in range(TOKEN_TILES):
+                    transpose_q(u, j)
+                    copy_q(u, j, engines[1 + j])
+            for u in (0, 1):
+                for j in range(TOKEN_TILES):
+                    den_matmuls(u, j)
+                    hs_matmuls(u, j)
+                den_guard(u)
+                den_recip(u)
+                normalise(u, 0, V)
+                normalise(u, 1, A)
+            for g in range(GROUPS):
+                transpose_wo(g)
+            for g in range(GROUPS):
+                copy_wo(g)
+            transpose_vk(2)
+            copy_vk(2, A)
+            transpose_q(2, 0)
+            copy_q(2, 0, V)
+            transpose_q(2, 1)
+            copy_q(2, 1, A)
+            transpose_vk(3)
+            copy_vk(3, V)
+            transpose_q(3, 0)
+            copy_q(3, 0, V)
+            transpose_q(3, 1)
+            copy_q(3, 1, V)
+            for g in range(GROUPS):
+                quantise_wo(g)
+            for u in (2, 3):
+                for j in range(TOKEN_TILES):
+                    den_matmuls(u, j)
+                    hs_matmuls(u, j)
+                den_guard(u)
+                den_recip(u)
+                normalise(u, 0, V)
+            normalise(2, 1, A)
+            normalise(3, 1, A)
+            order = [(u, j) for u in range(UNITS) for j in range(TOKEN_TILES)]
+            for u, j in order:
+                transpose_a(u, j)
+                copy_a(u, j, V if (u, j) in ((0, 0), (1, 0)) else A)
+            quantise_a(0, 0)
+            quantise_a(1, 0)
+            quantise_a(0, 1)
+            quantise_a(1, 1)
+            for u, j in order[4:]:
+                quantise_a(u, j)
+            for b in range(B):
+                for j in range(TOKEN_TILES):
+                    project(b, j)
+            for b in range(B):
+                for j in range(TOKEN_TILES):
+                    finish(b, j)

@@ -57,7 +57,7 @@ def tile_lineartransformerblock_pc_s_kernel(tc, q_feat, vk, k_sum, Wo, bo, out):
         zeros = keep.tile([P, P], F32)
         nc.vector.memset(zeros[:], 0.0)
         idle_ps = psum.tile([P, P], F32, tag="bank", bufs=BANKS, name="idle_ps")
-        for repeat in range(3):
+        for repeat in range(5):
             nc.tensor.matmul(out=idle_ps[:], lhsT=zeros[:], rhs=zeros[:], start=True, stop=True)
 
         ident = keep.tile([P, P], BF16)

@@ -32,7 +32,6 @@ def tile_lineartransformerblock_pc_s_kernel(tc, q_feat, vk, k_sum, Wo, bo, out):
     with tc.tile_pool(name="keep", bufs=1) as keep, tc.psum_pool(name="psum", bufs=1) as psum:
         ks_rows = keep.tile([P, D], BF16)
         nc.gpsimd.memset(ks_rows[:], 0.0)
-        nc.scalar.dma_start(out=ks_rows[0 : B * H, :], in_=k_sum.rearrange("b h d -> (b h) d"))
 
         vk_sb = [keep.tile([P, PACK, D], BF16, name="vk_sb%d" % u) for u in range(UNITS)]
         q_sb = [keep.tile([P, RUN, D], BF16, name="q_sb%d" % u) for u in range(UNITS)]
@@ -48,6 +47,7 @@ def tile_lineartransformerblock_pc_s_kernel(tc, q_feat, vk, k_sum, Wo, bo, out):
             nc.sync.dma_start(out=q_sb[u][:], in_=q_unit.rearrange("(p r) d -> p r d", r=RUN))
 
         load_unit(0)
+        nc.sync.dma_start(out=ks_rows[0 : B * H, :], in_=k_sum.rearrange("b h d -> (b h) d"))
         load_unit(1)
         nc.sync.dma_start(out=wo_sb[:], in_=Wo.rearrange("(p ct) k -> p ct k", ct=C_TILES))
         for u in range(2, UNITS):
@@ -69,10 +69,7 @@ def tile_lineartransformerblock_pc_s_kernel(tc, q_feat, vk, k_sum, Wo, bo, out):
             out=sort_f32[:].rearrange("k (p jj) -> k p jj", jj=PER), in_=ident_f32[:].rearrange("k (jj p) -> k p jj", jj=PER)
         )
 
-        ksT_ps = psum.tile([P, PACK * P], BF16, tag="bank", bufs=BANKS)
-        nc.tensor.transpose(ksT_ps[:, 0:P], ks_rows[:], ident[:])
         ksT = keep.tile([P, B * H], BF16)
-        nc.scalar.copy(out=ksT[:], in_=ksT_ps[:, 0 : B * H])
 
         vkT = [keep.tile([P, PACK, PACK, PH], BF16, name="vkT%d" % u) for u in range(UNITS)]
         qT = [keep.tile([P, TOKEN_TILES, PACK, PER, PH], BF16, name="qT%d" % u) for u in range(UNITS)]
@@ -87,6 +84,11 @@ def tile_lineartransformerblock_pc_s_kernel(tc, q_feat, vk, k_sum, Wo, bo, out):
         den = [keep.tile([P, TOKEN_TILES, PACK], F32, name="den%d" % u) for u in range(UNITS)]
         recip = [keep.tile([P, TOKEN_TILES, HALVES, PACK], F32, name="recip%d" % u) for u in range(UNITS)]
         vkT_ps, qT_ps, den_ps, hs_ps, aT_ps, woT_ps, out_ps = {}, {}, {}, {}, {}, {}, {}
+
+        def transpose_k_sum():
+            ksT_ps = psum.tile([P, P], BF16, tag="bank", bufs=BANKS)
+            nc.tensor.transpose(ksT_ps[:], ks_rows[:], ident[:])
+            nc.scalar.copy(out=ksT[:], in_=ksT_ps[:, 0 : B * H])
 
         def transpose_vk(u):
             vkT_ps[u] = psum.tile([P, PACK, PACK, PH], BF16, tag="bank", bufs=BANKS, name="vkT_ps")
@@ -121,7 +123,7 @@ def tile_lineartransformerblock_pc_s_kernel(tc, q_feat, vk, k_sum, Wo, bo, out):
                 nc.tensor.matmul(out=den_ps[u][:, j, h : h + 1], lhsT=queries(u, j, h), rhs=ksT[:, bh : bh + 1], start=True, stop=True)
 
         def den_guard(u):
-            nc.scalar.activation(out=den[u][:], in_=den_ps[u][:], func=COPY, bias=EPS)
+            nc.vector.tensor_scalar(out=den[u][:], in0=den_ps[u][:], scalar1=EPS, scalar2=None, op0=ADD)
 
         def den_recip(u):
             nc.vector.reciprocal(out=recip[u][:], in_=den[u][:].unsqueeze(2).to_broadcast([P, TOKEN_TILES, HALVES, PACK]))
@@ -182,10 +184,11 @@ def tile_lineartransformerblock_pc_s_kernel(tc, q_feat, vk, k_sum, Wo, bo, out):
                     every_second = wo_words[:, ct, HALVES * P * g + w : HALVES * P * (g + 1) : HALVES]
                     nc.tensor.transpose(woT_ps[g][:, w, ct, :], every_second, ident_f32[:])
 
-        def copy_wo(g):
-            nc.scalar.copy(
-                out=w_grouped[:, g].rearrange("n c t -> n (c t)").bitcast(F32).rearrange("n (p ct w) -> n p ct w", ct=C_TILES, w=HALVES),
-                in_=woT_ps[g][:].rearrange("n w ct p -> n p ct w"),
+        def copy_wo(g, engine):
+            copy(
+                engine,
+                w_grouped[:, g].rearrange("n c t -> n (c t)").bitcast(F32).rearrange("n (p ct w) -> n p ct w", ct=C_TILES, w=HALVES),
+                woT_ps[g][:].rearrange("n w ct p -> n p ct w"),
             )
 
         def quantise_wo(g):
@@ -207,19 +210,28 @@ def tile_lineartransformerblock_pc_s_kernel(tc, q_feat, vk, k_sum, Wo, bo, out):
                     stop=(g == GROUPS - 1),
                 )
 
-        def finish(b, j):
+        def finish(b, j, parts=1):
             out_sb = keep.tile([P, C], F32, name="out_sb%d%d" % (b, j))
-            nc.vector.tensor_tensor(out=out_sb[:], in0=out_ps[b, j][:], in1=bias[:], op=ADD)
-            nc.sync.dma_start(out=out[b].rearrange("(q j) c -> q j c", j=TOKEN_TILES)[:, j, :], in_=out_sb[:])
+            for part in range(parts):
+                cols = slice(part * C // parts, (part + 1) * C // parts)
+                nc.vector.tensor_tensor(out=out_sb[:, cols], in0=out_ps[b, j][:, cols], in1=bias[:, cols], op=ADD)
+                nc.sync.dma_start(out=out[b].rearrange("(q j) c -> q j c", j=TOKEN_TILES)[:, j, cols], in_=out_sb[:, cols])
 
         V, A = nc.vector, nc.scalar
         with tc.manual_schedule():
-            for u, engines in ((0, (A, V, A)), (1, (V, A, V))):
-                transpose_vk(u)
-                copy_vk(u, engines[0])
-                for j in range(TOKEN_TILES):
-                    transpose_q(u, j)
-                    copy_q(u, j, engines[1 + j])
+            transpose_vk(0)
+            copy_vk(0, A)
+            transpose_q(0, 0)
+            copy_q(0, 0, V)
+            transpose_q(0, 1)
+            transpose_k_sum()
+            copy_q(0, 1, A)
+            transpose_vk(1)
+            copy_vk(1, V)
+            transpose_q(1, 0)
+            copy_q(1, 0, A)
+            transpose_q(1, 1)
+            copy_q(1, 1, V)
             for u in (0, 1):
                 for j in range(TOKEN_TILES):
                     den_matmuls(u, j)
@@ -228,46 +240,39 @@ def tile_lineartransformerblock_pc_s_kernel(tc, q_feat, vk, k_sum, Wo, bo, out):
                 den_recip(u)
                 normalise(u, 0, V)
                 normalise(u, 1, A)
-            for g in range(GROUPS):
-                transpose_wo(g)
-            for g in range(GROUPS):
-                copy_wo(g)
-            transpose_vk(2)
-            copy_vk(2, A)
-            transpose_q(2, 0)
-            copy_q(2, 0, V)
-            transpose_q(2, 1)
-            copy_q(2, 1, A)
-            transpose_vk(3)
-            copy_vk(3, V)
-            transpose_q(3, 0)
-            copy_q(3, 0, V)
-            transpose_q(3, 1)
-            copy_q(3, 1, V)
-            for g in range(GROUPS):
+            transpose_wo(0)
+            copy_wo(0, V)
+            transpose_wo(1)
+            copy_wo(1, A)
+            for u, vk_engine, g in ((2, A, 0), (3, V, 1)):
+                transpose_vk(u)
+                copy_vk(u, vk_engine)
+                transpose_q(u, 0)
+                copy_q(u, 0, V)
+                transpose_q(u, 1)
+                copy_q(u, 1, A)
                 quantise_wo(g)
             for u in (2, 3):
-                for j in range(TOKEN_TILES):
-                    den_matmuls(u, j)
-                    hs_matmuls(u, j)
+                den_matmuls(u, 0)
+                den_matmuls(u, 1)
+                hs_matmuls(u, 0)
+                hs_matmuls(u, 1)
                 den_guard(u)
                 den_recip(u)
                 normalise(u, 0, V)
-            normalise(2, 1, A)
-            normalise(3, 1, A)
-            order = [(u, j) for u in range(UNITS) for j in range(TOKEN_TILES)]
-            for u, j in order:
+                normalise(u, 1, A)
+            tiles = [(u, j) for u in range(UNITS) for j in range(TOKEN_TILES)]
+            for u, j in tiles:
                 transpose_a(u, j)
-                copy_a(u, j, V if (u, j) in ((0, 0), (1, 0)) else A)
-            quantise_a(0, 0)
-            quantise_a(1, 0)
-            quantise_a(0, 1)
-            quantise_a(1, 1)
-            for u, j in order[4:]:
+                copy_a(u, j, V if u < 2 and j == 0 else A)
+            for u, j in tiles[:-1]:
                 quantise_a(u, j)
-            for b in range(B):
-                for j in range(TOKEN_TILES):
-                    project(b, j)
-            for b in range(B):
-                for j in range(TOKEN_TILES):
-                    finish(b, j)
+            project(0, 0)
+            project(0, 1)
+            finish(0, 0)
+            quantise_a(*tiles[-1])
+            project(1, 0)
+            project(1, 1)
+            finish(0, 1)
+            finish(1, 0)
+            finish(1, 1, parts=2)

@@ -123,7 +123,7 @@ def tile_lineartransformerblock_pc_s_kernel(tc, q_feat, vk, k_sum, Wo, bo, out):
                 nc.tensor.matmul(out=den_ps[u][:, j, h : h + 1], lhsT=queries(u, j, h), rhs=ksT[:, bh : bh + 1], start=True, stop=True)
 
         def den_guard(u):
-            nc.vector.tensor_scalar(out=den[u][:], in0=den_ps[u][:], scalar1=EPS, scalar2=None, op0=ADD)
+            nc.scalar.activation(out=den[u][:], in_=den_ps[u][:], func=COPY, bias=EPS)
 
         def den_recip(u):
             nc.vector.reciprocal(out=recip[u][:], in_=den[u][:].unsqueeze(2).to_broadcast([P, TOKEN_TILES, HALVES, PACK]))
@@ -237,6 +237,7 @@ def tile_lineartransformerblock_pc_s_kernel(tc, q_feat, vk, k_sum, Wo, bo, out):
                     den_matmuls(u, j)
                     hs_matmuls(u, j)
                 den_guard(u)
+            for u in (0, 1):
                 den_recip(u)
                 normalise(u, 0, V)
                 normalise(u, 1, A)
@@ -258,6 +259,7 @@ def tile_lineartransformerblock_pc_s_kernel(tc, q_feat, vk, k_sum, Wo, bo, out):
                 hs_matmuls(u, 0)
                 hs_matmuls(u, 1)
                 den_guard(u)
+            for u in (2, 3):
                 den_recip(u)
                 normalise(u, 0, V)
                 normalise(u, 1, A)
@@ -275,4 +277,4 @@ def tile_lineartransformerblock_pc_s_kernel(tc, q_feat, vk, k_sum, Wo, bo, out):
             project(1, 1)
             finish(0, 1)
             finish(1, 0)
-            finish(1, 1, parts=2)
+            finish(1, 1)

@@ -13,7 +13,7 @@ COPY = mybir.ActivationFunctionType.Copy
 P = 128
 PACK = 4
 B, H, S, D, C = 2, 8, 256, 128, 256
-EPS = 1e-15
+EPS_PARTS = (9 * 2.0**-53, 59 * 2.0**-66)
 GROUPS = H // PACK
 UNITS = B * GROUPS
 PH = P // PACK
@@ -23,6 +23,8 @@ PER = RUN // TOKEN_TILES
 C_TILES = C // P
 BANKS = 8
 HALVES = 2
+
+IDLE_COLUMNS = 120
 
 FLOPS = 2 * B * H * S * D * D + 2 * B * H * S * D + 2 * B * S * H * D * C
 
@@ -58,10 +60,16 @@ def tile_lineartransformerblock_pc_s_kernel(tc, q_feat, vk, k_sum, Wo, bo, out):
         nc.vector.memset(zeros[:], 0.0)
         idle_ps = psum.tile([P, P], F32, tag="bank", bufs=BANKS, name="idle_ps")
         for repeat in range(5):
-            nc.tensor.matmul(out=idle_ps[:], lhsT=zeros[:], rhs=zeros[:], start=True, stop=True)
+            nc.tensor.matmul(out=idle_ps[:, 0:IDLE_COLUMNS], lhsT=zeros[:], rhs=zeros[:, 0:IDLE_COLUMNS], start=True, stop=True)
 
         ident = keep.tile([P, P], BF16)
         make_identity(nc, ident[:])
+        ones = keep.tile([P, P], BF16)
+        nc.gpsimd.memset(ones[:], 1.0)
+        guard = keep.tile([P, TOKEN_TILES * PACK], BF16)
+        nc.gpsimd.memset(guard[:], 0.0)
+        for row, part in zip((0, 32), EPS_PARTS):
+            nc.gpsimd.memset(guard[row : row + 1, :], part)
         ident_f32 = keep.tile([P, P], F32)
         make_identity(nc, ident_f32[:])
         sort_f32 = keep.tile([P, P], F32)
@@ -81,7 +89,6 @@ def tile_lineartransformerblock_pc_s_kernel(tc, q_feat, vk, k_sum, Wo, bo, out):
         w_codes = keep.tile([P, GROUPS, C], U32, align_bytes=64)
         w_scales = keep.tile([P, GROUPS, C], U8, align_bytes=64)
 
-        den = [keep.tile([P, TOKEN_TILES, PACK], F32, name="den%d" % u) for u in range(UNITS)]
         recip = [keep.tile([P, TOKEN_TILES, HALVES, PACK], F32, name="recip%d" % u) for u in range(UNITS)]
         vkT_ps, qT_ps, den_ps, hs_ps, aT_ps, woT_ps, out_ps = {}, {}, {}, {}, {}, {}, {}
 
@@ -118,15 +125,14 @@ def tile_lineartransformerblock_pc_s_kernel(tc, q_feat, vk, k_sum, Wo, bo, out):
         def den_matmuls(u, j):
             if j == 0:
                 den_ps[u] = psum.tile([P, TOKEN_TILES, PACK], F32, tag="bank", bufs=BANKS, name="den_ps")
+                nc.tensor.matmul(out=den_ps[u][:].rearrange("p j h -> p (j h)"), lhsT=ones[:], rhs=guard[:], start=True, stop=False)
             for h in range(PACK):
                 bh = PACK * u + h
-                nc.tensor.matmul(out=den_ps[u][:, j, h : h + 1], lhsT=queries(u, j, h), rhs=ksT[:, bh : bh + 1], start=True, stop=True)
-
-        def den_guard(u):
-            nc.scalar.activation(out=den[u][:], in_=den_ps[u][:], func=COPY, bias=EPS)
+                last = j == TOKEN_TILES - 1 and h == PACK - 1
+                nc.tensor.matmul(out=den_ps[u][:, j, h : h + 1], lhsT=queries(u, j, h), rhs=ksT[:, bh : bh + 1], start=False, stop=last)
 
         def den_recip(u):
-            nc.vector.reciprocal(out=recip[u][:], in_=den[u][:].unsqueeze(2).to_broadcast([P, TOKEN_TILES, HALVES, PACK]))
+            nc.vector.reciprocal(out=recip[u][:], in_=den_ps[u][:].unsqueeze(2).to_broadcast([P, TOKEN_TILES, HALVES, PACK]))
 
         def hs_matmuls(u, j):
             hs_ps[u, j] = psum.tile([P, HALVES, PACK, HALVES, PH], F32, tag="bank", bufs=BANKS, name="hs_ps")
@@ -236,7 +242,6 @@ def tile_lineartransformerblock_pc_s_kernel(tc, q_feat, vk, k_sum, Wo, bo, out):
                 for j in range(TOKEN_TILES):
                     den_matmuls(u, j)
                     hs_matmuls(u, j)
-                den_guard(u)
             for u in (0, 1):
                 den_recip(u)
                 normalise(u, 0, V)
@@ -245,20 +250,18 @@ def tile_lineartransformerblock_pc_s_kernel(tc, q_feat, vk, k_sum, Wo, bo, out):
             copy_wo(0, V)
             transpose_wo(1)
             copy_wo(1, A)
-            for u, vk_engine, g in ((2, A, 0), (3, V, 1)):
+            for u, engines, g in ((2, (A, V, A), 0), (3, (V, A, A), 1)):
                 transpose_vk(u)
-                copy_vk(u, vk_engine)
-                transpose_q(u, 0)
-                copy_q(u, 0, V)
-                transpose_q(u, 1)
-                copy_q(u, 1, A)
+                copy_vk(u, engines[0])
+                for j in range(TOKEN_TILES):
+                    transpose_q(u, j)
+                    copy_q(u, j, engines[1 + j])
                 quantise_wo(g)
             for u in (2, 3):
                 den_matmuls(u, 0)
                 den_matmuls(u, 1)
                 hs_matmuls(u, 0)
                 hs_matmuls(u, 1)
-                den_guard(u)
             for u in (2, 3):
                 den_recip(u)
                 normalise(u, 0, V)

@@ -24,7 +24,7 @@ C_TILES = C // P
 BANKS = 8
 HALVES = 2
 
-IDLE_COLUMNS = 120
+LAST_IDLE = 120
 
 FLOPS = 2 * B * H * S * D * D + 2 * B * H * S * D + 2 * B * S * H * D * C
 
@@ -59,8 +59,12 @@ def tile_lineartransformerblock_pc_s_kernel(tc, q_feat, vk, k_sum, Wo, bo, out):
         zeros = keep.tile([P, P], F32)
         nc.vector.memset(zeros[:], 0.0)
         idle_ps = psum.tile([P, P], F32, tag="bank", bufs=BANKS, name="idle_ps")
-        for repeat in range(5):
-            nc.tensor.matmul(out=idle_ps[:, 0:IDLE_COLUMNS], lhsT=zeros[:], rhs=zeros[:, 0:IDLE_COLUMNS], start=True, stop=True)
+
+        def idle(columns):
+            nc.tensor.matmul(out=idle_ps[:, 0:columns], lhsT=zeros[:], rhs=zeros[:, 0:columns], start=True, stop=True)
+
+        for repeat in range(4):
+            idle(P)
 
         ident = keep.tile([P, P], BF16)
         make_identity(nc, ident[:])
@@ -227,6 +231,7 @@ def tile_lineartransformerblock_pc_s_kernel(tc, q_feat, vk, k_sum, Wo, bo, out):
         with tc.manual_schedule():
             transpose_vk(0)
             copy_vk(0, A)
+            idle(LAST_IDLE)
             transpose_q(0, 0)
             copy_q(0, 0, V)
             transpose_q(0, 1)
@@ -260,16 +265,20 @@ def tile_lineartransformerblock_pc_s_kernel(tc, q_feat, vk, k_sum, Wo, bo, out):
             for u in (2, 3):
                 den_matmuls(u, 0)
                 den_matmuls(u, 1)
+                if u == 3:
+                    transpose_a(0, 0)
                 hs_matmuls(u, 0)
                 hs_matmuls(u, 1)
             for u in (2, 3):
                 den_recip(u)
                 normalise(u, 0, V)
                 normalise(u, 1, A)
-            tiles = [(u, j) for u in range(UNITS) for j in range(TOKEN_TILES)]
-            for u, j in tiles:
+                if u == 2:
+                    copy_a(0, 0, A)
+            tiles = ((0, 0), (1, 0), (0, 1), (1, 1), (2, 0), (2, 1), (3, 0), (3, 1))
+            for u, j in tiles[1:]:
                 transpose_a(u, j)
-                copy_a(u, j, V if u < 2 and j == 0 else A)
+                copy_a(u, j, V if (u, j) in ((1, 0), (0, 1)) else A)
             for u, j in tiles[:-1]:
                 quantise_a(u, j)
             project(0, 0)

@@ -185,14 +185,18 @@ def tile_lineartransformerblock_pc_s_kernel(tc, q_feat, vk, k_sum, Wo, bo, out):
                 in_=a_grouped[u][:, j, :, :].rearrange("n q t -> n (q t)"),
             )
 
-        wo_words = wo_sb[:].bitcast(F32)
+        wo_words = keep.tile([P, C_TILES, GROUPS, HALVES, P], U32)
+        for g in range(GROUPS):
+            nc.gpsimd.tensor_copy(
+                out=wo_words[:, :, g],
+                in_=wo_sb[:].bitcast(U32)[:, :, HALVES * P * g : HALVES * P * (g + 1)].rearrange("p ct (x w) -> p ct w x", w=HALVES),
+            )
 
         def transpose_wo(g):
             woT_ps[g] = psum.tile([P, HALVES, C_TILES, P], F32, tag="bank", bufs=BANKS, name="woT_ps")
             for w in range(HALVES):
                 for ct in range(C_TILES):
-                    every_second = wo_words[:, ct, HALVES * P * g + w : HALVES * P * (g + 1) : HALVES]
-                    nc.tensor.transpose(woT_ps[g][:, w, ct, :], every_second, ident_f32[:])
+                    nc.tensor.transpose(woT_ps[g][:, w, ct, :], wo_words[:, ct, g, w].bitcast(F32), ident_f32[:])
 
         def copy_wo(g, engine):
             copy(
@@ -251,17 +255,24 @@ def tile_lineartransformerblock_pc_s_kernel(tc, q_feat, vk, k_sum, Wo, bo, out):
                 den_recip(u)
                 normalise(u, 0, V)
                 normalise(u, 1, A)
+            transpose_vk(2)
             transpose_wo(0)
             copy_wo(0, V)
+            copy_vk(2, A)
+            transpose_q(2, 0)
+            copy_q(2, 0, V)
+            transpose_q(2, 1)
+            copy_q(2, 1, A)
+            quantise_wo(0)
             transpose_wo(1)
             copy_wo(1, A)
-            for u, engines, g in ((2, (A, V, A), 0), (3, (V, A, A), 1)):
-                transpose_vk(u)
-                copy_vk(u, engines[0])
-                for j in range(TOKEN_TILES):
-                    transpose_q(u, j)
-                    copy_q(u, j, engines[1 + j])
-                quantise_wo(g)
+            transpose_vk(3)
+            copy_vk(3, V)
+            quantise_wo(1)
+            transpose_q(3, 0)
+            copy_q(3, 0, A)
+            transpose_q(3, 1)
+            copy_q(3, 1, A)
             for u in (2, 3):
                 den_matmuls(u, 0)
                 den_matmuls(u, 1)

import concourse.mybir as mybir
from concourse.masks import make_identity

F32 = mybir.dt.float32
BF16 = mybir.dt.bfloat16
U32 = mybir.dt.uint32
U8 = mybir.dt.uint8
FP8X4 = mybir.dt.float8_e4m3fn_x4
MULT = mybir.AluOpType.mult
ADD = mybir.AluOpType.add
COPY = mybir.ActivationFunctionType.Copy

P = 128
PACK = 4
B, H, S, D, C = 2, 8, 256, 128, 256
EPS_PARTS = (9 * 2.0**-53, 59 * 2.0**-66)
GROUPS = H // PACK
UNITS = B * GROUPS
PH = P // PACK
RUN = S // PH
TOKEN_TILES = S // P
PER = RUN // TOKEN_TILES
C_TILES = C // P
BANKS = 8
HALVES = 2

LAST_IDLE = 120

FLOPS = 2 * B * H * S * D * D + 2 * B * H * S * D + 2 * B * S * H * D * C


def tile_lineartransformerblock_pc_s_kernel(tc, q_feat, vk, k_sum, Wo, bo, out):
    nc = tc.nc
    with tc.tile_pool(name="keep", bufs=1) as keep, tc.psum_pool(name="psum", bufs=1) as psum:
        ks_rows = keep.tile([P, D], BF16)
        nc.gpsimd.memset(ks_rows[:], 0.0)

        vk_sb = [keep.tile([P, PACK, D], BF16, name="vk_sb%d" % u) for u in range(UNITS)]
        q_sb = [keep.tile([P, RUN, D], BF16, name="q_sb%d" % u) for u in range(UNITS)]
        wo_sb = keep.tile([P, C_TILES, H * D], BF16)
        bias = keep.tile([P, C], BF16)
        vk_rows = vk.rearrange("b h n d -> (b h n) d")
        q_rows = q_feat.rearrange("b h s d -> (b h s) d")

        def load_unit(u):
            vk_unit = vk_rows[PACK * D * u : PACK * D * (u + 1), :]
            nc.sync.dma_start(out=vk_sb[u][:], in_=vk_unit.rearrange("(p i) d -> p i d", i=PACK))
            q_unit = q_rows[PACK * S * u : PACK * S * (u + 1), :]
            nc.sync.dma_start(out=q_sb[u][:], in_=q_unit.rearrange("(p r) d -> p r d", r=RUN))

        load_unit(0)
        nc.sync.dma_start(out=ks_rows[0 : B * H, :], in_=k_sum.rearrange("b h d -> (b h) d"))
        load_unit(1)
        nc.sync.dma_start(out=wo_sb[:], in_=Wo.rearrange("(p ct) k -> p ct k", ct=C_TILES))
        for u in range(2, UNITS):
            load_unit(u)
        nc.sync.dma_start(out=bias[:], in_=bo.partition_broadcast(P))

        zeros = keep.tile([P, P], F32)
        nc.vector.memset(zeros[:], 0.0)
        idle_ps = psum.tile([P, P], F32, tag="bank", bufs=BANKS, name="idle_ps")

        def idle(columns):
            nc.tensor.matmul(out=idle_ps[:, 0:columns], lhsT=zeros[:], rhs=zeros[:, 0:columns], start=True, stop=True)

        for repeat in range(4):
            idle(P)

        ident = keep.tile([P, P], BF16)
        make_identity(nc, ident[:])
        ones = keep.tile([P, P], BF16)
        nc.gpsimd.memset(ones[:], 1.0)
        guard = keep.tile([P, TOKEN_TILES * PACK], BF16)
        nc.gpsimd.memset(guard[:], 0.0)
        for row, part in zip((0, 32), EPS_PARTS):
            nc.gpsimd.memset(guard[row : row + 1, :], part)
        ident_f32 = keep.tile([P, P], F32)
        make_identity(nc, ident_f32[:])
        sort_f32 = keep.tile([P, P], F32)
        nc.gpsimd.tensor_copy(
            out=sort_f32[:].rearrange("k (p jj) -> k p jj", jj=PER), in_=ident_f32[:].rearrange("k (jj p) -> k p jj", jj=PER)
        )

        ksT = keep.tile([P, B * H], BF16)

        vkT = [keep.tile([P, PACK, PACK, PH], BF16, name="vkT%d" % u) for u in range(UNITS)]
        qT = [keep.tile([P, TOKEN_TILES, PACK, PER, PH], BF16, name="qT%d" % u) for u in range(UNITS)]
        a_sb = [keep.tile([P, TOKEN_TILES, HALVES, PACK * D // HALVES], BF16, name="a_sb%d" % u) for u in range(UNITS)]
        a_grouped = [keep.tile([P, TOKEN_TILES, P, PACK], BF16, name="a_grouped%d" % u, align_bytes=64) for u in range(UNITS)]
        a_codes = [keep.tile([P, TOKEN_TILES, P], U32, name="a_codes%d" % u, align_bytes=64) for u in range(UNITS)]
        a_scales = [keep.tile([P, TOKEN_TILES, P], U8, name="a_scales%d" % u, align_bytes=64) for u in range(UNITS)]
        w_grouped = keep.tile([P, GROUPS, C, PACK], BF16, align_bytes=64)
        w_codes = keep.tile([P, GROUPS, C], U32, align_bytes=64)
        w_scales = keep.tile([P, GROUPS, C], U8, align_bytes=64)

        recip = [keep.tile([P, TOKEN_TILES, HALVES, PACK], F32, name="recip%d" % u) for u in range(UNITS)]
        vkT_ps, qT_ps, den_ps, hs_ps, aT_ps, woT_ps, out_ps = {}, {}, {}, {}, {}, {}, {}

        def transpose_k_sum():
            ksT_ps = psum.tile([P, P], BF16, tag="bank", bufs=BANKS)
            nc.tensor.transpose(ksT_ps[:], ks_rows[:], ident[:])
            nc.scalar.copy(out=ksT[:], in_=ksT_ps[:, 0 : B * H])

        def transpose_vk(u):
            vkT_ps[u] = psum.tile([P, PACK, PACK, PH], BF16, tag="bank", bufs=BANKS, name="vkT_ps")
            for i in range(PACK):
                nc.tensor.transpose(vkT_ps[u][:, :, i, :], vk_sb[u][:, i, :], ident[:])

        def copy(engine, out, in_):
            if engine is nc.scalar:
                nc.scalar.copy(out=out, in_=in_)
            else:
                nc.vector.tensor_copy(out=out, in_=in_)

        def copy_vk(u, engine):
            copy(engine, vkT[u][:], vkT_ps[u][:])

        def transpose_q(u, j):
            qT_ps[u, j] = psum.tile([P, PACK, PER, PH], BF16, tag="bank", bufs=BANKS, name="qT_ps")
            for jj in range(PER):
                nc.tensor.transpose(qT_ps[u, j][:, :, jj, :], q_sb[u][:, TOKEN_TILES * jj + j, :], ident[:])

        def copy_q(u, j, engine):
            copy(engine, qT[u][:, j], qT_ps[u, j][:])

        def queries(u, j, h):
            return qT[u][:, j, h].rearrange("d jj p -> d (jj p)")

        def den_matmuls(u, j):
            if j == 0:
                den_ps[u] = psum.tile([P, TOKEN_TILES, PACK], F32, tag="bank", bufs=BANKS, name="den_ps")
                nc.tensor.matmul(out=den_ps[u][:].rearrange("p j h -> p (j h)"), lhsT=ones[:], rhs=guard[:], start=True, stop=False)
            for h in range(PACK):
                bh = PACK * u + h
                last = j == TOKEN_TILES - 1 and h == PACK - 1
                nc.tensor.matmul(out=den_ps[u][:, j, h : h + 1], lhsT=queries(u, j, h), rhs=ksT[:, bh : bh + 1], start=False, stop=last)

        def den_recip(u):
            nc.vector.reciprocal(out=recip[u][:], in_=den_ps[u][:].unsqueeze(2).to_broadcast([P, TOKEN_TILES, HALVES, PACK]))

        def hs_matmuls(u, j):
            hs_ps[u, j] = psum.tile([P, HALVES, PACK, HALVES, PH], F32, tag="bank", bufs=BANKS, name="hs_ps")
            for h in range(PACK):
                nc.tensor.matmul(
                    out=hs_ps[u, j][:, :, h, :, :],
                    lhsT=queries(u, j, h),
                    rhs=vkT[u][:, h].rearrange("d (w e) m -> d w e m", w=HALVES),
                    start=True,
                    stop=True,
                )

        def normalise(u, j, engine):
            if engine is nc.scalar:
                for h in range(PACK):
                    nc.scalar.activation(
                        out=a_sb[u][:, j].rearrange("p w (h m e) -> p w h m e", h=PACK, e=HALVES)[:, :, h],
                        in_=hs_ps[u, j][:, :, h].rearrange("p w e m -> p w m e"),
                        func=COPY,
                        scale=recip[u][:, j, 0, h : h + 1],
                    )
                return
            nc.vector.tensor_tensor(
                out=a_sb[u][:, j].rearrange("p w (h m e) -> p (w h) m e", h=PACK, e=HALVES),
                in0=hs_ps[u, j][:].rearrange("p w h e m -> p (w h) m e"),
                in1=recip[u][:, j].rearrange("p w h -> p (w h)").unsqueeze(2).unsqueeze(3).to_broadcast([P, HALVES * PACK, PH, HALVES]),
                op=MULT,
            )

        def transpose_a(u, j):
            aT_ps[u, j] = psum.tile([P, HALVES, P], F32, tag="bank", bufs=BANKS, name="aT_ps")
            for w in range(HALVES):
                nc.tensor.transpose(aT_ps[u, j][:, w, :], a_sb[u][:, j, w, :].bitcast(F32), sort_f32[:])

        def copy_a(u, j, engine):
            copy(
                engine,
                a_grouped[u][:, j].rearrange("n q t -> n (q t)").bitcast(F32).rearrange("n (q w) -> n q w", w=HALVES),
                aT_ps[u, j][:].rearrange("n w q -> n q w"),
            )

        def quantise_a(u, j):
            nc.vector.quantize_mx(
                out=a_codes[u][:, j, :].bitcast(FP8X4),
                scales=a_scales[u][:, j, :],
                in_=a_grouped[u][:, j, :, :].rearrange("n q t -> n (q t)"),
            )

        wo_words = keep.tile([P, C_TILES, GROUPS, HALVES, P], U32)
        for g in range(GROUPS):
            nc.gpsimd.tensor_copy(
                out=wo_words[:, :, g],
                in_=wo_sb[:].bitcast(U32)[:, :, HALVES * P * g : HALVES * P * (g + 1)].rearrange("p ct (x w) -> p ct w x", w=HALVES),
            )

        def transpose_wo(g):
            woT_ps[g] = psum.tile([P, HALVES, C_TILES, P], F32, tag="bank", bufs=BANKS, name="woT_ps")
            for w in range(HALVES):
                for ct in range(C_TILES):
                    nc.tensor.transpose(woT_ps[g][:, w, ct, :], wo_words[:, ct, g, w].bitcast(F32), ident_f32[:])

        def copy_wo(g, engine):
            copy(
                engine,
                w_grouped[:, g].rearrange("n c t -> n (c t)").bitcast(F32).rearrange("n (p ct w) -> n p ct w", ct=C_TILES, w=HALVES),
                woT_ps[g][:].rearrange("n w ct p -> n p ct w"),
            )

        def quantise_wo(g):
            nc.vector.quantize_mx(
                out=w_codes[:, g].bitcast(FP8X4), scales=w_scales[:, g], in_=w_grouped[:, g].rearrange("n c t -> n (c t)")
            )

        def project(b, j):
            out_ps[b, j] = psum.tile([P, C], F32, tag="bank", bufs=BANKS, name="out_ps")
            for g in range(GROUPS):
                u = GROUPS * b + g
                nc.tensor.matmul_mx(
                    out=out_ps[b, j][:],
                    lhsT=a_codes[u][:, j, :].bitcast(FP8X4),
                    lhsT_scale=a_scales[u][:, j, :],
                    rhs=w_codes[:, g, :].bitcast(FP8X4),
                    rhs_scale=w_scales[:, g, :],
                    start=(g == 0),
                    stop=(g == GROUPS - 1),
                )

        def finish(b, j, parts=1):
            out_sb = keep.tile([P, C], F32, name="out_sb%d%d" % (b, j))
            for part in range(parts):
                cols = slice(part * C // parts, (part + 1) * C // parts)
                nc.vector.tensor_tensor(out=out_sb[:, cols], in0=out_ps[b, j][:, cols], in1=bias[:, cols], op=ADD)
                nc.sync.dma_start(out=out[b].rearrange("(q j) c -> q j c", j=TOKEN_TILES)[:, j, cols], in_=out_sb[:, cols])

        V, A = nc.vector, nc.scalar
        with tc.manual_schedule():
            transpose_vk(0)
            copy_vk(0, A)
            idle(LAST_IDLE)
            transpose_q(0, 0)
            copy_q(0, 0, V)
            transpose_q(0, 1)
            transpose_k_sum()
            copy_q(0, 1, A)
            transpose_vk(1)
            copy_vk(1, V)
            transpose_q(1, 0)
            copy_q(1, 0, A)
            transpose_q(1, 1)
            copy_q(1, 1, V)
            for u in (0, 1):
                for j in range(TOKEN_TILES):
                    den_matmuls(u, j)
                    hs_matmuls(u, j)
            for u in (0, 1):
                den_recip(u)
                normalise(u, 0, V)
                normalise(u, 1, A)
            transpose_vk(2)
            transpose_wo(0)
            copy_wo(0, V)
            copy_vk(2, A)
            transpose_q(2, 0)
            copy_q(2, 0, V)
            transpose_q(2, 1)
            copy_q(2, 1, A)
            quantise_wo(0)
            transpose_wo(1)
            copy_wo(1, A)
            transpose_vk(3)
            copy_vk(3, V)
            quantise_wo(1)
            transpose_q(3, 0)
            copy_q(3, 0, A)
            transpose_q(3, 1)
            copy_q(3, 1, A)
            for u in (2, 3):
                den_matmuls(u, 0)
                den_matmuls(u, 1)
                if u == 3:
                    transpose_a(0, 0)
                hs_matmuls(u, 0)
                hs_matmuls(u, 1)
            for u in (2, 3):
                den_recip(u)
                normalise(u, 0, V)
                normalise(u, 1, A)
                if u == 2:
                    copy_a(0, 0, A)
            tiles = ((0, 0), (1, 0), (0, 1), (1, 1), (2, 0), (2, 1), (3, 0), (3, 1))
            for u, j in tiles[1:]:
                transpose_a(u, j)
                copy_a(u, j, V if (u, j) in ((1, 0), (0, 1)) else A)
            for u, j in tiles[:-1]:
                quantise_a(u, j)
            project(0, 0)
            project(0, 1)
            finish(0, 0)
            quantise_a(*tiles[-1])
            project(1, 0)
            project(1, 1)
            finish(0, 1)
            finish(1, 0)
            finish(1, 1)
